import numpy as np
import ml_dtypes


def mxq(x, axis, fmt="e4m3"):
    dtype, down = {"e4m3": (ml_dtypes.float8_e4m3fn, 7), "e5m2": (ml_dtypes.float8_e5m2, 14)}[fmt]
    v = np.moveaxis(np.asarray(x, np.float32).astype(ml_dtypes.bfloat16).astype(np.float64), axis, -1)
    blocks = v.reshape(v.shape[:-1] + (-1, 32))
    amax = np.abs(blocks).max(-1, keepdims=True)
    byte = np.maximum(np.where(amax > 0, np.frexp(amax)[1] - 1 + 127, 0) - down, 1)
    scale = np.exp2(byte - 127.0)
    codes = (blocks / scale).astype(np.float32).astype(dtype).astype(np.float64)
    return np.moveaxis((codes * scale).reshape(v.shape), -1, axis)


WIDE = False


def mx_kscale(k):
    if not WIDE:
        return np.ones(k)
    levels = np.array([10, -10, 5, -5, 0])
    a = np.random.permutation(np.resize(levels, k // 512 * 4)).reshape(k // 512, 4)
    idx = np.arange(k)
    return np.exp2(a[idx // 512, idx % 128 // 32])


BF16 = ml_dtypes.bfloat16


def bf(x):
    return np.asarray(x, np.float32).astype(BF16)


def f64(x):
    return np.asarray(x).astype(np.float64)


N, K, F, NB = 1024, 512, 384, 32
EPS = 1e-6


def erf(v):
    a = np.minimum(np.abs(v), 6.0)
    term = a.copy()
    total = a.copy()
    for n in range(1, 130):
        term = term * (2.0 * a * a / (2.0 * n + 1.0))
        total = total + term
    return np.sign(v) * (2.0 / np.sqrt(np.pi)) * np.exp(-a * a) * total


def gelu(v):
    return 0.5 * v * (1.0 + erf(v / np.sqrt(2.0)))


def setup_inputs():
    s = mx_kscale(K)
    edge = np.random.random_sample((N, N)) < NB / N
    return {"x": bf(np.random.standard_normal((N, K)) * s),
            "adj": bf(np.random.random_sample((N, N)) * edge),
            "W1": bf(np.random.standard_normal((K, F)) * 3.0 / np.sqrt(K) / s[:, None]),
            "b1": bf(np.random.standard_normal(F) * 0.3),
            "ln_gamma": bf(1.0 + 0.1 * np.random.standard_normal(F)),
            "ln_beta": bf(0.1 * np.random.standard_normal(F))}


def reference(x, adj, W1, b1, ln_gamma, ln_beta):
    a = f64(adj)
    h = (mxq(f64(x), 1, "e4m3") @ mxq(f64(W1), 0, "e4m3")) + f64(b1)
    deg = a.sum(axis=1) + 1.0
    dinv = np.where(deg > 0, deg ** -0.5, 0.0)
    hs = dinv[:, None] * h
    agg = (mxq(a, 1, "e4m3") @ mxq(hs, 0, "e4m3")) + hs
    g = gelu(dinv[:, None] * agg)
    mu = g.mean(axis=-1, keepdims=True)
    var = ((g - mu) ** 2).mean(axis=-1, keepdims=True)
    return (g - mu) / np.sqrt(var + EPS) * f64(ln_gamma) + f64(ln_beta)

@@ -1,0 +1,247 @@
+from contextlib import ExitStack
+
+import concourse.bass as bass
+import concourse.mybir as mybir
+import concourse.tile as tile
+from concourse.masks import make_identity
+
+F32 = mybir.dt.float32
+BF16 = mybir.dt.bfloat16
+U32 = mybir.dt.uint32
+U8 = mybir.dt.uint8
+FP8X4 = mybir.dt.float8_e4m3fn_x4
+ALU = mybir.AluOpType
+ACT = mybir.ActivationFunctionType
+
+P = 128
+N = 1024
+K = 512
+F = 384
+EPS = 1e-6
+NCH = 4
+FSPLIT = ((0, 256), (256, 128))
+
+FLOPS = 2 * N * K * F + 2 * N * N * F
+
+
+def tile_gcnlayer_pa_kernel(tc, x, adj, W1, b1, ln_gamma, ln_beta, out):
+    nc = tc.nc
+    with ExitStack() as ctx:
+        keep = ctx.enter_context(tc.tile_pool(name="keep", bufs=1))
+        work = ctx.enter_context(tc.tile_pool(name="work", bufs=3))
+        ps_t = ctx.enter_context(tc.psum_pool(name="ps_t", bufs=3))
+        ps_h = ctx.enter_context(tc.psum_pool(name="ps_h", bufs=2))
+        ps_o = ctx.enter_context(tc.psum_pool(name="ps_o", bufs=3))
+
+        vec = keep.tile([P, 3, 512], BF16)
+        nc.vector.memset(vec[:], 0.0)
+        ones = keep.tile([P, P], BF16)
+        nc.vector.memset(ones[:], 1.0)
+        neghalf = keep.tile([P, 4], F32)
+        nc.vector.memset(neghalf[:], -0.5)
+        ident = keep.tile([P, P], F32)
+        make_identity(nc, ident[:])
+
+        nc.scalar.dma_start(out=vec[0:1, 0, 0:F], in_=b1.unsqueeze(0))
+        nc.scalar.dma_start(out=vec[0:1, 1, 0:F], in_=ln_gamma.unsqueeze(0))
+        nc.scalar.dma_start(out=vec[0:1, 2, 0:F], in_=ln_beta.unsqueeze(0))
+
+        w1_sb = keep.tile([P, 4, F], BF16)
+        nc.sync.dma_start(
+            out=w1_sb[:].rearrange("p (u e) f -> p u e f", u=2),
+            in_=W1.rearrange("(u p e) f -> p u e f", u=2, e=2),
+        )
+        x_sb = []
+        for c in range(NCH):
+            xt = keep.tile([P, 2 * K], BF16, name="x_sb%d" % c)
+            nc.sync.dma_start(
+                out=xt[:].rearrange("p (e k) -> p e k", e=2),
+                in_=x[256 * c : 256 * (c + 1), :].rearrange("(p e) k -> p e k", e=2),
+            )
+            x_sb.append(xt)
+        a_sb = []
+        for c in range(NCH):
+            at = keep.tile([P, 2 * N], BF16, name="a_sb%d" % c)
+            nc.sync.dma_start(
+                out=at[:].rearrange("p (e j) -> p e j", e=2),
+                in_=adj[256 * c : 256 * (c + 1), :].rearrange("(p e) j -> p e j", e=2),
+            )
+            a_sb.append(at)
+
+        w1g = keep.tile([P, F, 4], BF16, align_bytes=64)
+        nc.vector.tensor_copy(out=w1g[:], in_=w1_sb[:].rearrange("p t f -> p f t"))
+        w1q = keep.tile([P, F], U32, align_bytes=64)
+        w1s = keep.tile([P, F], U8, align_bytes=64)
+        for f0, fn in FSPLIT:
+            nc.vector.quantize_mx(
+                out=w1q[:, f0 : f0 + fn].bitcast(FP8X4),
+                scales=w1s[:, f0 : f0 + fn],
+                in_=w1g[:, f0 : f0 + fn, :].rearrange("p f t -> p (f t)"),
+            )
+
+        vbc = keep.tile([P, 3, F], F32)
+        for v in range(3):
+            pb = ps_o.tile([P, 512], F32, tag="o", name="pb%d" % v)
+            nc.tensor.matmul(out=pb[:], lhsT=ones[:], rhs=vec[:, v, :], start=True, stop=True)
+            nc.scalar.copy(out=vbc[:, v, :], in_=pb[:, 0:F])
+
+        xq = keep.tile([P, N], U32, align_bytes=64)
+        xs = keep.tile([P, N], U8, align_bytes=64)
+        T = keep.tile([P, 8, F], F32)
+        for c in range(NCH):
+            xw = x_sb[c][:].bitcast(F32)
+            pt = ps_t.tile([P, 512], F32, tag="t", name="ptx%d" % c)
+            for b in range(4):
+                nc.tensor.transpose(
+                    out=pt[:, 128 * b : 128 * (b + 1)],
+                    in_=xw[:, 128 * b : 128 * (b + 1)],
+                    identity=ident[:],
+                )
+            xg = work.tile([P, 1024], BF16, align_bytes=64, tag="xg", name="xg%d" % c)
+            nc.scalar.copy(
+                out=xg[:].bitcast(F32).rearrange("p (e j u) -> p e j u", e=2, u=2),
+                in_=pt[:].rearrange("p (e u j) -> p e j u", e=2, u=2),
+            )
+            nc.vector.quantize_mx(
+                out=xq[:, 256 * c : 256 * (c + 1)].bitcast(FP8X4),
+                scales=xs[:, 256 * c : 256 * (c + 1)],
+                in_=xg[:],
+            )
+            for e in range(2):
+                jt = 2 * c + e
+                ph = ps_h.tile([P, 512], F32, tag="h", name="ph%d" % jt)
+                for f0, fn in FSPLIT:
+                    nc.tensor.matmul_mx(
+                        out=ph[:, f0 : f0 + fn],
+                        lhsT=xq[:, 128 * jt : 128 * (jt + 1)].bitcast(FP8X4),
+                        lhsT_scale=xs[:, 128 * jt : 128 * (jt + 1)],
+                        rhs=w1q[:, f0 : f0 + fn].bitcast(FP8X4),
+                        rhs_scale=w1s[:, f0 : f0 + fn],
+                        start=True,
+                        stop=True,
+                    )
+                nc.vector.tensor_tensor(out=T[:, jt, :], in0=ph[:, 0:F], in1=vbc[:, 0, :], op=ALU.add)
+
+        aq = keep.tile([P, 2 * N], U32, align_bytes=64)
+        asc = keep.tile([P, 2 * N], U8, align_bytes=64)
+        hq = keep.tile([P, 2 * F], U32, align_bytes=64)
+        hsc = keep.tile([P, 2 * F], U8, align_bytes=64)
+        degv = keep.tile([P, NCH], F32)
+        degs = keep.tile([P, NCH], F32)
+        d1 = keep.tile([P, NCH, 2], F32)
+        dinv = keep.tile([P, 8], F32)
+        for c in range(NCH):
+            junkv = work.tile([P, N], BF16, tag="junkv", name="junkv%d" % c)
+            nc.vector.tensor_scalar(
+                out=junkv[:], in0=a_sb[c][:, 0:N], scalar1=1.0, scalar2=None,
+                op0=ALU.mult, op1=ALU.add, accum_out=degv[:, c : c + 1],
+            )
+            junks = work.tile([P, N], BF16, tag="junks", name="junks%d" % c)
+            nc.scalar.activation(
+                out=junks[:], in_=a_sb[c][:, N : 2 * N], func=ACT.Copy, accum_out=degs[:, c : c + 1],
+            )
+            aw = a_sb[c][:].bitcast(F32)
+            for e in range(2):
+                it = 2 * c + e
+                pt = ps_t.tile([P, 512], F32, tag="t", name="pta%d" % it)
+                for b in range(4):
+                    nc.tensor.transpose(
+                        out=pt[:, 128 * b : 128 * (b + 1)],
+                        in_=aw[:, 512 * e + 128 * b : 512 * e + 128 * (b + 1)],
+                        identity=ident[:],
+                    )
+                ag = work.tile([P, 1024], BF16, align_bytes=64, tag="ag", name="ag%d" % it)
+                nc.scalar.copy(
+                    out=ag[:].bitcast(F32).rearrange("p (g i u) -> p g i u", g=2, u=2),
+                    in_=pt[:].rearrange("p (g u i) -> p g i u", g=2, u=2),
+                )
+                nc.vector.quantize_mx(
+                    out=aq[:, 256 * it : 256 * (it + 1)].bitcast(FP8X4),
+                    scales=asc[:, 256 * it : 256 * (it + 1)],
+                    in_=ag[:],
+                )
+            if c % 2 == 1:
+                g = c // 2
+                nc.gpsimd.tensor_scalar(
+                    out=d1[:, 2 * g : 2 * g + 2, 0], in0=degv[:, 2 * g : 2 * g + 2],
+                    scalar1=1.0, scalar2=1.0, op0=ALU.mult, op1=ALU.add,
+                )
+                nc.gpsimd.tensor_scalar(
+                    out=d1[:, 2 * g : 2 * g + 2, 1], in0=degs[:, 2 * g : 2 * g + 2],
+                    scalar1=1.0, scalar2=1.0, op0=ALU.mult, op1=ALU.add,
+                )
+                nc.gpsimd.tensor_tensor(
+                    out=dinv[:, 4 * g : 4 * g + 4],
+                    in0=d1[:, 2 * g : 2 * g + 2, :].rearrange("p c e -> p (c e)"),
+                    in1=neghalf[:], op=ALU.pow,
+                )
+                hsb = work.tile([P, F, 4], BF16, align_bytes=64, tag="hsb", name="hsb%d" % g)
+                nc.vector.tensor_tensor(
+                    out=hsb[:],
+                    in0=T[:, 4 * g : 4 * g + 4, :].rearrange("p t f -> p f t"),
+                    in1=dinv[:, 4 * g : 4 * g + 4].unsqueeze(1).to_broadcast([P, F, 4]),
+                    op=ALU.mult,
+                )
+                for f0, fn in FSPLIT:
+                    nc.vector.quantize_mx(
+                        out=hq[:, F * g + f0 : F * g + f0 + fn].bitcast(FP8X4),
+                        scales=hsc[:, F * g + f0 : F * g + f0 + fn],
+                        in_=hsb[:, f0 : f0 + fn, :].rearrange("p f t -> p (f t)"),
+                    )
+
+        sumg = keep.tile([P, 8], F32)
+        ssq = keep.tile([P, 8], F32)
+        negmu = keep.tile([P, 8], F32)
+        vare = keep.tile([P, 8], F32)
+        rstd = keep.tile([P, 8], F32)
+        out_v = out.rearrange("(c p e) f -> p c e f", c=NCH, e=2)
+        for it in range(8):
+            po = ps_o.tile([P, 512], F32, tag="o", name="po%d" % it)
+            for f0, fn in FSPLIT:
+                for g in range(2):
+                    a0 = 256 * it + 128 * g
+                    nc.tensor.matmul_mx(
+                        out=po[:, f0 : f0 + fn],
+                        lhsT=aq[:, a0 : a0 + 128].bitcast(FP8X4),
+                        lhsT_scale=asc[:, a0 : a0 + 128],
+                        rhs=hq[:, F * g + f0 : F * g + f0 + fn].bitcast(FP8X4),
+                        rhs_scale=hsc[:, F * g + f0 : F * g + f0 + fn],
+                        start=(g == 0),
+                        stop=(g == 1),
+                    )
+            col = slice(it, it + 1)
+            s = work.tile([P, F], F32, tag="s", name="s%d" % it)
+            nc.vector.scalar_tensor_tensor(
+                out=s[:], in0=T[:, it, :], scalar=dinv[:, col], in1=po[:, 0:F],
+                op0=ALU.mult, op1=ALU.add,
+            )
+            gl = work.tile([P, F], F32, tag="gl", name="gl%d" % it)
+            nc.scalar.activation(
+                out=gl[:], in_=s[:], func=ACT.Gelu, scale=dinv[:, col], accum_out=sumg[:, col],
+            )
+            nc.gpsimd.tensor_scalar(
+                out=negmu[:, col], in0=sumg[:, col], scalar1=-1.0 / F, scalar2=0.0,
+                op0=ALU.mult, op1=ALU.add,
+            )
+            sq = work.tile([P, F], F32, tag="sq", name="sq%d" % it)
+            nc.scalar.activation(
+                out=sq[:], in_=gl[:], func=ACT.Square, bias=negmu[:, col], accum_out=ssq[:, col],
+            )
+            nc.gpsimd.tensor_scalar(
+                out=vare[:, col], in0=ssq[:, col], scalar1=1.0 / F, scalar2=EPS,
+                op0=ALU.mult, op1=ALU.add,
+            )
+            nc.gpsimd.tensor_tensor(
+                out=rstd[:, col], in0=vare[:, col], in1=neghalf[:, 0:1], op=ALU.pow,
+            )
+            w = work.tile([P, F], F32, tag="w", name="w%d" % it)
+            nc.vector.scalar_tensor_tensor(
+                out=w[:], in0=gl[:], scalar=negmu[:, col], in1=vbc[:, 1, :],
+                op0=ALU.add, op1=ALU.mult,
+            )
+            o = work.tile([P, F], F32, tag="o_sb", name="o%d" % it)
+            nc.vector.scalar_tensor_tensor(
+                out=o[:], in0=w[:], scalar=rstd[:, col], in1=vbc[:, 2, :],
+                op0=ALU.mult, op1=ALU.add,
+            )
+            nc.sync.dma_start(out=out_v[:, it // 2, it % 2, :], in_=o[:])

@@ -1,8 +1,6 @@
 from contextlib import ExitStack
 
-import concourse.bass as bass
 import concourse.mybir as mybir
-import concourse.tile as tile
 from concourse.masks import make_identity
 
 F32 = mybir.dt.float32
@@ -19,7 +17,10 @@ K = 512
 F = 384
 EPS = 1e-6
 NCH = 4
+NT = 8
+APITCH = 1040
 FSPLIT = ((0, 256), (256, 128))
+V_DEG_CHUNKS = (2, 3)
 
 FLOPS = 2 * N * K * F + 2 * N * N * F
 
@@ -27,24 +28,26 @@ FLOPS = 2 * N * K * F + 2 * N * N * F
 def tile_gcnlayer_pa_kernel(tc, x, adj, W1, b1, ln_gamma, ln_beta, out):
     nc = tc.nc
     with ExitStack() as ctx:
+        ctx.enter_context(tc.manual_schedule())
         keep = ctx.enter_context(tc.tile_pool(name="keep", bufs=1))
-        work = ctx.enter_context(tc.tile_pool(name="work", bufs=3))
-        ps_t = ctx.enter_context(tc.psum_pool(name="ps_t", bufs=3))
-        ps_h = ctx.enter_context(tc.psum_pool(name="ps_h", bufs=2))
+        junk = ctx.enter_context(tc.tile_pool(name="junk", bufs=2))
+        ps_t = ctx.enter_context(tc.psum_pool(name="ps_t", bufs=5))
         ps_o = ctx.enter_context(tc.psum_pool(name="ps_o", bufs=3))
 
         vec = keep.tile([P, 3, 512], BF16)
         nc.vector.memset(vec[:], 0.0)
-        ones = keep.tile([P, P], BF16)
-        nc.vector.memset(ones[:], 1.0)
         neghalf = keep.tile([P, 4], F32)
         nc.vector.memset(neghalf[:], -0.5)
+        ones = keep.tile([P, P], BF16)
+        nc.vector.memset(ones[:], 1.0)
         ident = keep.tile([P, P], F32)
         make_identity(nc, ident[:])
 
         nc.scalar.dma_start(out=vec[0:1, 0, 0:F], in_=b1.unsqueeze(0))
         nc.scalar.dma_start(out=vec[0:1, 1, 0:F], in_=ln_gamma.unsqueeze(0))
         nc.scalar.dma_start(out=vec[0:1, 2, 0:F], in_=ln_beta.unsqueeze(0))
+        warm = keep.tile([P, 1], F32)
+        nc.scalar.activation(out=warm[:], in_=neghalf[:, 0:1], func=ACT.Gelu)
 
         w1_sb = keep.tile([P, 4, F], BF16)
         nc.sync.dma_start(
@@ -61,9 +64,11 @@ def tile_gcnlayer_pa_kernel(tc, x, adj, W1, b1, ln_gamma, ln_beta, out):
             x_sb.append(xt)
         a_sb = []
         for c in range(NCH):
-            at = keep.tile([P, 2 * N], BF16, name="a_sb%d" % c)
+            at = keep.tile([P, 2, APITCH], BF16, name="a_sb%d" % c)
+            if c not in V_DEG_CHUNKS:
+                nc.vector.memset(at[:, :, N : N + 1], 1.0)
             nc.sync.dma_start(
-                out=at[:].rearrange("p (e j) -> p e j", e=2),
+                out=at[:, :, 0:N],
                 in_=adj[256 * c : 256 * (c + 1), :].rearrange("(p e) j -> p e j", e=2),
             )
             a_sb.append(at)
@@ -87,115 +92,126 @@ def tile_gcnlayer_pa_kernel(tc, x, adj, W1, b1, ln_gamma, ln_beta, out):
 
         xq = keep.tile([P, N], U32, align_bytes=64)
         xs = keep.tile([P, N], U8, align_bytes=64)
-        T = keep.tile([P, 8, F], F32)
-        for c in range(NCH):
-            xw = x_sb[c][:].bitcast(F32)
-            pt = ps_t.tile([P, 512], F32, tag="t", name="ptx%d" % c)
-            for b in range(4):
-                nc.tensor.transpose(
-                    out=pt[:, 128 * b : 128 * (b + 1)],
-                    in_=xw[:, 128 * b : 128 * (b + 1)],
-                    identity=ident[:],
-                )
-            xg = work.tile([P, 1024], BF16, align_bytes=64, tag="xg", name="xg%d" % c)
-            nc.scalar.copy(
-                out=xg[:].bitcast(F32).rearrange("p (e j u) -> p e j u", e=2, u=2),
-                in_=pt[:].rearrange("p (e u j) -> p e j u", e=2, u=2),
-            )
-            nc.vector.quantize_mx(
-                out=xq[:, 256 * c : 256 * (c + 1)].bitcast(FP8X4),
-                scales=xs[:, 256 * c : 256 * (c + 1)],
-                in_=xg[:],
-            )
-            for e in range(2):
-                jt = 2 * c + e
-                ph = ps_h.tile([P, 512], F32, tag="h", name="ph%d" % jt)
-                for f0, fn in FSPLIT:
-                    nc.tensor.matmul_mx(
-                        out=ph[:, f0 : f0 + fn],
-                        lhsT=xq[:, 128 * jt : 128 * (jt + 1)].bitcast(FP8X4),
-                        lhsT_scale=xs[:, 128 * jt : 128 * (jt + 1)],
-                        rhs=w1q[:, f0 : f0 + fn].bitcast(FP8X4),
-                        rhs_scale=w1s[:, f0 : f0 + fn],
-                        start=True,
-                        stop=True,
-                    )
-                nc.vector.tensor_tensor(out=T[:, jt, :], in0=ph[:, 0:F], in1=vbc[:, 0, :], op=ALU.add)
-
+        T = keep.tile([P, NT, F], F32)
         aq = keep.tile([P, 2 * N], U32, align_bytes=64)
         asc = keep.tile([P, 2 * N], U8, align_bytes=64)
         hq = keep.tile([P, 2 * F], U32, align_bytes=64)
         hsc = keep.tile([P, 2 * F], U8, align_bytes=64)
-        degv = keep.tile([P, NCH], F32)
-        degs = keep.tile([P, NCH], F32)
-        d1 = keep.tile([P, NCH, 2], F32)
-        dinv = keep.tile([P, 8], F32)
-        for c in range(NCH):
-            junkv = work.tile([P, N], BF16, tag="junkv", name="junkv%d" % c)
-            nc.vector.tensor_scalar(
-                out=junkv[:], in0=a_sb[c][:, 0:N], scalar1=1.0, scalar2=None,
-                op0=ALU.mult, op1=ALU.add, accum_out=degv[:, c : c + 1],
-            )
-            junks = work.tile([P, N], BF16, tag="junks", name="junks%d" % c)
-            nc.scalar.activation(
-                out=junks[:], in_=a_sb[c][:, N : 2 * N], func=ACT.Copy, accum_out=degs[:, c : c + 1],
-            )
-            aw = a_sb[c][:].bitcast(F32)
-            for e in range(2):
-                it = 2 * c + e
-                pt = ps_t.tile([P, 512], F32, tag="t", name="pta%d" % it)
-                for b in range(4):
-                    nc.tensor.transpose(
-                        out=pt[:, 128 * b : 128 * (b + 1)],
-                        in_=aw[:, 512 * e + 128 * b : 512 * e + 128 * (b + 1)],
-                        identity=ident[:],
-                    )
-                ag = work.tile([P, 1024], BF16, align_bytes=64, tag="ag", name="ag%d" % it)
-                nc.scalar.copy(
-                    out=ag[:].bitcast(F32).rearrange("p (g i u) -> p g i u", g=2, u=2),
-                    in_=pt[:].rearrange("p (g u i) -> p g i u", g=2, u=2),
-                )
-                nc.vector.quantize_mx(
-                    out=aq[:, 256 * it : 256 * (it + 1)].bitcast(FP8X4),
-                    scales=asc[:, 256 * it : 256 * (it + 1)],
-                    in_=ag[:],
-                )
-            if c % 2 == 1:
-                g = c // 2
-                nc.gpsimd.tensor_scalar(
-                    out=d1[:, 2 * g : 2 * g + 2, 0], in0=degv[:, 2 * g : 2 * g + 2],
-                    scalar1=1.0, scalar2=1.0, op0=ALU.mult, op1=ALU.add,
-                )
-                nc.gpsimd.tensor_scalar(
-                    out=d1[:, 2 * g : 2 * g + 2, 1], in0=degs[:, 2 * g : 2 * g + 2],
-                    scalar1=1.0, scalar2=1.0, op0=ALU.mult, op1=ALU.add,
-                )
-                nc.gpsimd.tensor_tensor(
-                    out=dinv[:, 4 * g : 4 * g + 4],
-                    in0=d1[:, 2 * g : 2 * g + 2, :].rearrange("p c e -> p (c e)"),
-                    in1=neghalf[:], op=ALU.pow,
-                )
-                hsb = work.tile([P, F, 4], BF16, align_bytes=64, tag="hsb", name="hsb%d" % g)
-                nc.vector.tensor_tensor(
-                    out=hsb[:],
-                    in0=T[:, 4 * g : 4 * g + 4, :].rearrange("p t f -> p f t"),
-                    in1=dinv[:, 4 * g : 4 * g + 4].unsqueeze(1).to_broadcast([P, F, 4]),
-                    op=ALU.mult,
-                )
-                for f0, fn in FSPLIT:
-                    nc.vector.quantize_mx(
-                        out=hq[:, F * g + f0 : F * g + f0 + fn].bitcast(FP8X4),
-                        scales=hsc[:, F * g + f0 : F * g + f0 + fn],
-                        in_=hsb[:, f0 : f0 + fn, :].rearrange("p f t -> p (f t)"),
-                    )
-
-        sumg = keep.tile([P, 8], F32)
-        ssq = keep.tile([P, 8], F32)
-        negmu = keep.tile([P, 8], F32)
-        vare = keep.tile([P, 8], F32)
-        rstd = keep.tile([P, 8], F32)
+        deg1 = [keep.tile([P, 2], F32, name="deg1_%d" % c) for c in range(NCH)]
+        dinv = keep.tile([P, NT], F32)
+        sumg = keep.tile([P, NT], F32)
+        ssq = keep.tile([P, NT], F32)
+        negmu = keep.tile([P, NT], F32)
+        vare = keep.tile([P, NT], F32)
+        rstd = keep.tile([P, NT], F32)
         out_v = out.rearrange("(c p e) f -> p c e f", c=NCH, e=2)
-        for it in range(8):
+        pts = {}
+        xgs = {}
+        ags = {}
+        phs = {}
+        hsbs = {}
+        pos = {}
+        ss = {}
+        gls = {}
+        ws = {}
+
+        def xT(c):
+            xw = x_sb[c][:].bitcast(F32)
+            pt = ps_t.tile([P, 512], F32, tag="t", name="ptx%d" % c)
+            for b in range(4):
+                nc.tensor.transpose(out=pt[:, 128 * b : 128 * (b + 1)], in_=xw[:, 128 * b : 128 * (b + 1)], identity=ident[:])
+            pts[("x", c)] = pt
+
+        def xe(c):
+            xg = keep.tile([P, 1024], BF16, align_bytes=64, name="xg%d" % c)
+            nc.scalar.copy(
+                out=xg[:].bitcast(F32).rearrange("p (e j u) -> p e j u", e=2, u=2),
+                in_=pts[("x", c)][:].rearrange("p (e u j) -> p e j u", e=2, u=2),
+            )
+            xgs[c] = xg
+
+        def xqz(c):
+            nc.vector.quantize_mx(
+                out=xq[:, 256 * c : 256 * (c + 1)].bitcast(FP8X4),
+                scales=xs[:, 256 * c : 256 * (c + 1)],
+                in_=xgs[c][:],
+            )
+
+        def mm1(jt):
+            ph = ps_t.tile([P, 512], F32, tag="t", name="ph%d" % jt)
+            for f0, fn in FSPLIT:
+                nc.tensor.matmul_mx(
+                    out=ph[:, f0 : f0 + fn],
+                    lhsT=xq[:, 128 * jt : 128 * (jt + 1)].bitcast(FP8X4),
+                    lhsT_scale=xs[:, 128 * jt : 128 * (jt + 1)],
+                    rhs=w1q[:, f0 : f0 + fn].bitcast(FP8X4),
+                    rhs_scale=w1s[:, f0 : f0 + fn],
+                    start=True,
+                    stop=True,
+                )
+            phs[jt] = ph
+
+        def tp(jt):
+            nc.vector.tensor_tensor(out=T[:, jt, :], in0=phs[jt][:, 0:F], in1=vbc[:, 0, :], op=ALU.add)
+
+        def aT(it):
+            aw = a_sb[it // 2][:].bitcast(F32)
+            pt = ps_t.tile([P, 512], F32, tag="t", name="pta%d" % it)
+            for b in range(4):
+                nc.tensor.transpose(out=pt[:, 128 * b : 128 * (b + 1)], in_=aw[:, it % 2, 128 * b : 128 * (b + 1)], identity=ident[:])
+            pts[("a", it)] = pt
+
+        def ae(it):
+            ag = keep.tile([P, 1024], BF16, align_bytes=64, name="ag%d" % it)
+            nc.scalar.copy(
+                out=ag[:].bitcast(F32).rearrange("p (g i u) -> p g i u", g=2, u=2),
+                in_=pts[("a", it)][:].rearrange("p (g u i) -> p g i u", g=2, u=2),
+            )
+            ags[it] = ag
+
+        def aqz(it):
+            nc.vector.quantize_mx(
+                out=aq[:, 256 * it : 256 * (it + 1)].bitcast(FP8X4),
+                scales=asc[:, 256 * it : 256 * (it + 1)],
+                in_=ags[it][:],
+            )
+
+        def deg(it):
+            c, e = it // 2, it % 2
+            if c in V_DEG_CHUNKS:
+                jv = junk.tile([P, N], BF16, tag="jv", name="jv%d" % it)
+                nc.vector.tensor_scalar(
+                    out=jv[:], in0=a_sb[c][:, e, 0:N], scalar1=1.0, scalar2=1.0,
+                    op0=ALU.mult, op1=ALU.add, accum_out=deg1[c][:, e : e + 1],
+                )
+            else:
+                js = junk.tile([P, N + 1], BF16, tag="js", name="js%d" % it)
+                nc.scalar.activation(
+                    out=js[:], in_=a_sb[c][:, e, 0 : N + 1], func=ACT.Copy, accum_out=deg1[c][:, e : e + 1],
+                )
+
+        def dpow(c):
+            nc.gpsimd.tensor_tensor(out=dinv[:, 2 * c : 2 * c + 2], in0=deg1[c][:], in1=neghalf[:, 0:2], op=ALU.pow)
+
+        def f2(g):
+            hsb = keep.tile([P, F, 4], BF16, align_bytes=64, name="hsb%d" % g)
+            nc.vector.tensor_tensor(
+                out=hsb[:],
+                in0=T[:, 4 * g : 4 * g + 4, :].rearrange("p t f -> p f t"),
+                in1=dinv[:, 4 * g : 4 * g + 4].unsqueeze(1).to_broadcast([P, F, 4]),
+                op=ALU.mult,
+            )
+            hsbs[g] = hsb
+
+        def hqz(g):
+            for f0, fn in FSPLIT:
+                nc.vector.quantize_mx(
+                    out=hq[:, F * g + f0 : F * g + f0 + fn].bitcast(FP8X4),
+                    scales=hsc[:, F * g + f0 : F * g + f0 + fn],
+                    in_=hsbs[g][:, f0 : f0 + fn, :].rearrange("p f t -> p (f t)"),
+                )
+
+        def mm2(it):
             po = ps_o.tile([P, 512], F32, tag="o", name="po%d" % it)
             for f0, fn in FSPLIT:
                 for g in range(2):
@@ -209,39 +225,82 @@ def tile_gcnlayer_pa_kernel(tc, x, adj, W1, b1, ln_gamma, ln_beta, out):
                         start=(g == 0),
                         stop=(g == 1),
                     )
-            col = slice(it, it + 1)
-            s = work.tile([P, F], F32, tag="s", name="s%d" % it)
+            pos[it] = po
+
+        def e1(it):
+            s = keep.tile([P, F], F32, name="s%d" % it)
             nc.vector.scalar_tensor_tensor(
-                out=s[:], in0=T[:, it, :], scalar=dinv[:, col], in1=po[:, 0:F],
+                out=s[:], in0=T[:, it, :], scalar=dinv[:, it : it + 1], in1=pos[it][:, 0:F],
                 op0=ALU.mult, op1=ALU.add,
             )
-            gl = work.tile([P, F], F32, tag="gl", name="gl%d" % it)
+            ss[it] = s
+
+        def eg(it):
+            gl = keep.tile([P, F], F32, name="gl%d" % it)
             nc.scalar.activation(
-                out=gl[:], in_=s[:], func=ACT.Gelu, scale=dinv[:, col], accum_out=sumg[:, col],
+                out=gl[:], in_=ss[it][:], func=ACT.Gelu, scale=dinv[:, it : it + 1], accum_out=sumg[:, it : it + 1],
             )
+            gls[it] = gl
+
+        def emu(it):
             nc.gpsimd.tensor_scalar(
-                out=negmu[:, col], in0=sumg[:, col], scalar1=-1.0 / F, scalar2=0.0,
+                out=negmu[:, it : it + 1], in0=sumg[:, it : it + 1], scalar1=-1.0 / F, scalar2=0.0,
                 op0=ALU.mult, op1=ALU.add,
             )
-            sq = work.tile([P, F], F32, tag="sq", name="sq%d" % it)
+
+        def eq(it):
+            sq = junk.tile([P, F], F32, tag="sq", name="sq%d" % it)
             nc.scalar.activation(
-                out=sq[:], in_=gl[:], func=ACT.Square, bias=negmu[:, col], accum_out=ssq[:, col],
+                out=sq[:], in_=gls[it][:], func=ACT.Square, scale=-float(F), bias=sumg[:, it : it + 1],
+                accum_out=ssq[:, it : it + 1],
             )
+
+        def er(it):
             nc.gpsimd.tensor_scalar(
-                out=vare[:, col], in0=ssq[:, col], scalar1=1.0 / F, scalar2=EPS,
+                out=vare[:, it : it + 1], in0=ssq[:, it : it + 1], scalar1=1.0 / (float(F) ** 3), scalar2=EPS,
                 op0=ALU.mult, op1=ALU.add,
             )
-            nc.gpsimd.tensor_tensor(
-                out=rstd[:, col], in0=vare[:, col], in1=neghalf[:, 0:1], op=ALU.pow,
-            )
-            w = work.tile([P, F], F32, tag="w", name="w%d" % it)
+            nc.gpsimd.tensor_tensor(out=rstd[:, it : it + 1], in0=vare[:, it : it + 1], in1=neghalf[:, 0:1], op=ALU.pow)
+
+        def e4(it):
+            w = keep.tile([P, F], F32, name="w%d" % it)
             nc.vector.scalar_tensor_tensor(
-                out=w[:], in0=gl[:], scalar=negmu[:, col], in1=vbc[:, 1, :],
+                out=w[:], in0=gls[it][:], scalar=negmu[:, it : it + 1], in1=vbc[:, 1, :],
                 op0=ALU.add, op1=ALU.mult,
             )
-            o = work.tile([P, F], F32, tag="o_sb", name="o%d" % it)
+            ws[it] = w
+
+        def e5(it):
+            o = keep.tile([P, F], F32, name="o%d" % it)
             nc.vector.scalar_tensor_tensor(
-                out=o[:], in0=w[:], scalar=rstd[:, col], in1=vbc[:, 2, :],
+                out=o[:], in0=ws[it][:], scalar=rstd[:, it : it + 1], in1=vbc[:, 2, :],
                 op0=ALU.mult, op1=ALU.add,
             )
             nc.sync.dma_start(out=out_v[:, it // 2, it % 2, :], in_=o[:])
+
+        xT(0); xe(0); xT(1); xe(1)
+        xqz(0); mm1(0); mm1(1)
+        xT(2); xe(2); xqz(1); tp(0); tp(1); mm1(2); mm1(3)
+        xT(3); xe(3); xqz(2); tp(2); tp(3); mm1(4); mm1(5)
+        xqz(3); tp(4); tp(5); mm1(6); mm1(7); tp(6); tp(7)
+
+        aT(0); aT(1); deg(0); deg(1); dpow(0); ae(0)
+        aT(2); aT(3); deg(2); deg(3); dpow(1); ae(1)
+        deg(4); deg(5); dpow(2); deg(6); deg(7); dpow(3)
+        aT(4); aqz(0); aqz(1)
+        ae(2); aT(5); ae(3); aT(6); aT(7)
+        f2(0); hqz(0); f2(1); hqz(1); aqz(2); aqz(3)
+
+        for p in range(NT + 3):
+            if p < NT:
+                mm2(p)
+            if p + 4 < NT:
+                ae(p + 4)
+            if p < NT:
+                e1(p); eg(p); emu(p)
+            if p + 4 < NT:
+                aqz(p + 4)
+            if 0 <= p - 1 < NT:
+                eq(p - 1); er(p - 1); e4(p - 1)
+            if 0 <= p - 3 < NT:
+                e5(p - 3)

@@ -38,6 +38,8 @@ def tile_gcnlayer_pa_kernel(tc, x, adj, W1, b1, ln_gamma, ln_beta, out):
         nc.vector.memset(vec[:], 0.0)
         neghalf = keep.tile([P, 4], F32)
         nc.vector.memset(neghalf[:], -0.5)
+        ones_f = keep.tile([P, 1], F32)
+        nc.vector.memset(ones_f[:], 1.0)
         ones = keep.tile([P, P], BF16)
         nc.vector.memset(ones[:], 1.0)
         ident = keep.tile([P, P], F32)
@@ -47,7 +49,7 @@ def tile_gcnlayer_pa_kernel(tc, x, adj, W1, b1, ln_gamma, ln_beta, out):
         nc.scalar.dma_start(out=vec[0:1, 1, 0:F], in_=ln_gamma.unsqueeze(0))
         nc.scalar.dma_start(out=vec[0:1, 2, 0:F], in_=ln_beta.unsqueeze(0))
         warm = keep.tile([P, 1], F32)
-        nc.scalar.activation(out=warm[:], in_=neghalf[:, 0:1], func=ACT.Gelu)
+        nc.scalar.activation(out=warm[:], in_=ones_f[:, 0:1], func=ACT.Sqrt)
 
         w1_sb = keep.tile([P, 4, F], BF16)
         nc.sync.dma_start(
@@ -97,7 +99,9 @@ def tile_gcnlayer_pa_kernel(tc, x, adj, W1, b1, ln_gamma, ln_beta, out):
         asc = keep.tile([P, 2 * N], U8, align_bytes=64)
         hq = keep.tile([P, 2 * F], U32, align_bytes=64)
         hsc = keep.tile([P, 2 * F], U8, align_bytes=64)
-        deg1 = [keep.tile([P, 2], F32, name="deg1_%d" % c) for c in range(NCH)]
+        deg1 = [keep.tile([P, 4], F32, name="deg1_%d" % g) for g in range(2)]
+        sdeg = [keep.tile([P, 4], F32, name="sdeg%d" % g) for g in range(2)]
+        warm2 = keep.tile([P, 1], F32)
         dinv = keep.tile([P, NT], F32)
         sumg = keep.tile([P, NT], F32)
         ssq = keep.tile([P, NT], F32)
@@ -182,16 +186,19 @@ def tile_gcnlayer_pa_kernel(tc, x, adj, W1, b1, ln_gamma, ln_beta, out):
                 jv = junk.tile([P, N], BF16, tag="jv", name="jv%d" % it)
                 nc.vector.tensor_scalar(
                     out=jv[:], in0=a_sb[c][:, e, 0:N], scalar1=1.0, scalar2=1.0,
-                    op0=ALU.mult, op1=ALU.add, accum_out=deg1[c][:, e : e + 1],
+                    op0=ALU.mult, op1=ALU.add, accum_out=deg1[it // 4][:, it % 4 : it % 4 + 1],
                 )
             else:
                 js = junk.tile([P, N + 1], BF16, tag="js", name="js%d" % it)
                 nc.scalar.activation(
-                    out=js[:], in_=a_sb[c][:, e, 0 : N + 1], func=ACT.Copy, accum_out=deg1[c][:, e : e + 1],
+                    out=js[:], in_=a_sb[c][:, e, 0 : N + 1], func=ACT.Copy, accum_out=deg1[it // 4][:, it % 4 : it % 4 + 1],
                 )
 
-        def dpow(c):
-            nc.gpsimd.tensor_tensor(out=dinv[:, 2 * c : 2 * c + 2], in0=deg1[c][:], in1=neghalf[:, 0:2], op=ALU.pow)
+        def dsq(g):
+            nc.scalar.activation(out=sdeg[g][:], in_=deg1[g][:], func=ACT.Sqrt)
+
+        def drc(g):
+            nc.vector.reciprocal(out=dinv[:, 4 * g : 4 * g + 4], in_=sdeg[g][:])
 
         def f2(g):
             hsb = keep.tile([P, F, 4], BF16, align_bytes=64, name="hsb%d" % g)
@@ -255,12 +262,13 @@ def tile_gcnlayer_pa_kernel(tc, x, adj, W1, b1, ln_gamma, ln_beta, out):
                 accum_out=ssq[:, it : it + 1],
             )
 
-        def er(it):
+        def er(h):
+            cols = slice(4 * h, 4 * h + 4)
             nc.gpsimd.tensor_scalar(
-                out=vare[:, it : it + 1], in0=ssq[:, it : it + 1], scalar1=1.0 / (float(F) ** 3), scalar2=EPS,
+                out=vare[:, cols], in0=ssq[:, cols], scalar1=1.0 / (float(F) ** 3), scalar2=EPS,
                 op0=ALU.mult, op1=ALU.add,
             )
-            nc.gpsimd.tensor_tensor(out=rstd[:, it : it + 1], in0=vare[:, it : it + 1], in1=neghalf[:, 0:1], op=ALU.pow)
+            nc.gpsimd.tensor_tensor(out=rstd[:, cols], in0=vare[:, cols], in1=neghalf[:], op=ALU.pow)
 
         def e4(it):
             w = keep.tile([P, F], F32, name="w%d" % it)
@@ -284,14 +292,16 @@ def tile_gcnlayer_pa_kernel(tc, x, adj, W1, b1, ln_gamma, ln_beta, out):
         xT(3); xe(3); xqz(2); tp(2); tp(3); mm1(4); mm1(5)
         xqz(3); tp(4); tp(5); mm1(6); mm1(7); tp(6); tp(7)
 
-        aT(0); aT(1); deg(0); deg(1); dpow(0); ae(0)
-        aT(2); aT(3); deg(2); deg(3); dpow(1); ae(1)
-        deg(4); deg(5); dpow(2); deg(6); deg(7); dpow(3)
+        aT(0); aT(1); deg(0); deg(1); ae(0)
+        aT(2); aT(3); deg(2); deg(3); ae(1); dsq(0)
+        deg(4); deg(5); deg(6); deg(7); drc(0)
         aT(4); aqz(0); aqz(1)
-        ae(2); aT(5); ae(3); aT(6); aT(7)
-        f2(0); hqz(0); f2(1); hqz(1); aqz(2); aqz(3)
+        ae(2); aT(5); dsq(1)
+        nc.scalar.activation(out=warm2[:], in_=ones_f[:, 0:1], func=ACT.Gelu)
+        ae(3); aT(6); aT(7)
+        f2(0); hqz(0); drc(1); f2(1); hqz(1); aqz(2); aqz(3)
 
-        for p in range(NT + 3):
+        for p in range(NT + 1):
             if p < NT:
                 mm2(p)
             if p + 4 < NT:
@@ -301,6 +311,8 @@ def tile_gcnlayer_pa_kernel(tc, x, adj, W1, b1, ln_gamma, ln_beta, out):
             if p + 4 < NT:
                 aqz(p + 4)
             if 0 <= p - 1 < NT:
-                eq(p - 1); er(p - 1); e4(p - 1)
-            if 0 <= p - 3 < NT:
-                e5(p - 3)
+                eq(p - 1); e4(p - 1)
+                if p % 4 == 0:
+                    er(p // 4 - 1)
+        for it in range(NT):
+            e5(it)

@@ -20,7 +20,8 @@ NCH = 4
 NT = 8
 APITCH = 1040
 FSPLIT = ((0, 256), (256, 128))
-V_DEG_CHUNKS = (2, 3)
+LAG4 = 3
+LAG5 = 5
 
 FLOPS = 2 * N * K * F + 2 * N * N * F
 
@@ -67,8 +68,7 @@ def tile_gcnlayer_pa_kernel(tc, x, adj, W1, b1, ln_gamma, ln_beta, out):
         a_sb = []
         for c in range(NCH):
             at = keep.tile([P, 2, APITCH], BF16, name="a_sb%d" % c)
-            if c not in V_DEG_CHUNKS:
-                nc.vector.memset(at[:, :, N : N + 1], 1.0)
+            nc.vector.memset(at[:, :, N : N + 1], 1.0)
             nc.sync.dma_start(
                 out=at[:, :, 0:N],
                 in_=adj[256 * c : 256 * (c + 1), :].rearrange("(p e) j -> p e j", e=2),
@@ -87,10 +87,15 @@ def tile_gcnlayer_pa_kernel(tc, x, adj, W1, b1, ln_gamma, ln_beta, out):
             )
 
         vbc = keep.tile([P, 3, F], F32)
-        for v in range(3):
+        pbs = {}
+
+        def bcm(v):
             pb = ps_o.tile([P, 512], F32, tag="o", name="pb%d" % v)
             nc.tensor.matmul(out=pb[:], lhsT=ones[:], rhs=vec[:, v, :], start=True, stop=True)
-            nc.scalar.copy(out=vbc[:, v, :], in_=pb[:, 0:F])
+            pbs[v] = pb
+
+        def bce(v):
+            nc.scalar.copy(out=vbc[:, v, :], in_=pbs[v][:, 0:F])
 
         xq = keep.tile([P, N], U32, align_bytes=64)
         xs = keep.tile([P, N], U8, align_bytes=64)
@@ -99,8 +104,9 @@ def tile_gcnlayer_pa_kernel(tc, x, adj, W1, b1, ln_gamma, ln_beta, out):
         asc = keep.tile([P, 2 * N], U8, align_bytes=64)
         hq = keep.tile([P, 2 * F], U32, align_bytes=64)
         hsc = keep.tile([P, 2 * F], U8, align_bytes=64)
-        deg1 = [keep.tile([P, 4], F32, name="deg1_%d" % g) for g in range(2)]
-        sdeg = [keep.tile([P, 4], F32, name="sdeg%d" % g) for g in range(2)]
+        deg_s = [keep.tile([P, 2], F32, name="deg_s%d" % g) for g in range(2)]
+        deg_v = [keep.tile([P, 2], F32, name="deg_v%d" % g) for g in range(2)]
+        sdeg = keep.tile([P, NCH, 2], F32)
         warm2 = keep.tile([P, 1], F32)
         dinv = keep.tile([P, NT], F32)
         sumg = keep.tile([P, NT], F32)
@@ -182,23 +188,26 @@ def tile_gcnlayer_pa_kernel(tc, x, adj, W1, b1, ln_gamma, ln_beta, out):
 
         def deg(it):
             c, e = it // 2, it % 2
-            if c in V_DEG_CHUNKS:
+            if e == 1:
                 jv = junk.tile([P, N], BF16, tag="jv", name="jv%d" % it)
                 nc.vector.tensor_scalar(
                     out=jv[:], in0=a_sb[c][:, e, 0:N], scalar1=1.0, scalar2=1.0,
-                    op0=ALU.mult, op1=ALU.add, accum_out=deg1[it // 4][:, it % 4 : it % 4 + 1],
+                    op0=ALU.mult, op1=ALU.add, accum_out=deg_v[c // 2][:, c % 2 : c % 2 + 1],
                 )
             else:
                 js = junk.tile([P, N + 1], BF16, tag="js", name="js%d" % it)
                 nc.scalar.activation(
-                    out=js[:], in_=a_sb[c][:, e, 0 : N + 1], func=ACT.Copy, accum_out=deg1[it // 4][:, it % 4 : it % 4 + 1],
+                    out=js[:], in_=a_sb[c][:, e, 0 : N + 1], func=ACT.Copy, accum_out=deg_s[c // 2][:, c % 2 : c % 2 + 1],
                 )
 
         def dsq(g):
-            nc.scalar.activation(out=sdeg[g][:], in_=deg1[g][:], func=ACT.Sqrt)
+            nc.scalar.activation(out=sdeg[:, 2 * g : 2 * g + 2, 0], in_=deg_s[g][:], func=ACT.Sqrt)
+            nc.scalar.activation(out=sdeg[:, 2 * g : 2 * g + 2, 1], in_=deg_v[g][:], func=ACT.Sqrt)
 
         def drc(g):
-            nc.vector.reciprocal(out=dinv[:, 4 * g : 4 * g + 4], in_=sdeg[g][:])
+            nc.vector.reciprocal(
+                out=dinv[:, 4 * g : 4 * g + 4], in_=sdeg[:, 2 * g : 2 * g + 2, :].rearrange("p c e -> p (c e)")
+            )
 
         def f2(g):
             hsb = keep.tile([P, F, 4], BF16, align_bytes=64, name="hsb%d" % g)
@@ -263,12 +272,12 @@ def tile_gcnlayer_pa_kernel(tc, x, adj, W1, b1, ln_gamma, ln_beta, out):
             )
 
         def er(h):
-            cols = slice(4 * h, 4 * h + 4)
+            cols = slice(2 * h, 2 * h + 2)
             nc.gpsimd.tensor_scalar(
                 out=vare[:, cols], in0=ssq[:, cols], scalar1=1.0 / (float(F) ** 3), scalar2=EPS,
                 op0=ALU.mult, op1=ALU.add,
             )
-            nc.gpsimd.tensor_tensor(out=rstd[:, cols], in0=vare[:, cols], in1=neghalf[:], op=ALU.pow)
+            nc.gpsimd.tensor_tensor(out=rstd[:, cols], in0=vare[:, cols], in1=neghalf[:, 0:2], op=ALU.pow)
 
         def e4(it):
             w = keep.tile([P, F], F32, name="w%d" % it)
@@ -286,33 +295,30 @@ def tile_gcnlayer_pa_kernel(tc, x, adj, W1, b1, ln_gamma, ln_beta, out):
             )
             nc.sync.dma_start(out=out_v[:, it // 2, it % 2, :], in_=o[:])
 
-        xT(0); xe(0); xT(1); xe(1)
-        xqz(0); mm1(0); mm1(1)
-        xT(2); xe(2); xqz(1); tp(0); tp(1); mm1(2); mm1(3)
-        xT(3); xe(3); xqz(2); tp(2); tp(3); mm1(4); mm1(5)
-        xqz(3); tp(4); tp(5); mm1(6); mm1(7); tp(6); tp(7)
-
-        aT(0); aT(1); deg(0); deg(1); ae(0)
-        aT(2); aT(3); deg(2); deg(3); ae(1); dsq(0)
-        deg(4); deg(5); deg(6); deg(7); drc(0)
-        aT(4); aqz(0); aqz(1)
-        ae(2); aT(5); dsq(1)
+        xT(0); xT(1); xe(0); xe(1); bcm(0); bce(0); xT(2); xT(3); xe(2); xe(3)
+        xqz(0); xqz(1); mm1(0); mm1(1); mm1(2); mm1(3)
+        deg(1); xqz(2); tp(0); xqz(3); tp(1)
+        aT(0); mm1(4); mm1(5); mm1(6); mm1(7)
+        deg(0); deg(2); deg(3); dsq(0)
+        tp(2); tp(3); tp(4); tp(5); deg(5); tp(6); tp(7); deg(7)
+        ae(0); deg(4); deg(6); dsq(1)
+        aT(1); aT(2); bcm(1); bcm(2); aT(3); aT(4); aT(5)
+        ae(1); ae(2); aT(6); aT(7)
         nc.scalar.activation(out=warm2[:], in_=ones_f[:, 0:1], func=ACT.Gelu)
-        ae(3); aT(6); aT(7)
-        f2(0); hqz(0); drc(1); f2(1); hqz(1); aqz(2); aqz(3)
+        ae(3); bce(1); bce(2); ae(4); ae(5); ae(6); ae(7)
+        drc(0); f2(0); hqz(0); drc(1); f2(1); hqz(1)
+        aqz(0); aqz(1); aqz(2); aqz(3)
 
-        for p in range(NT + 1):
+        for p in range(NT + LAG5):
             if p < NT:
-                mm2(p)
-            if p + 4 < NT:
-                ae(p + 4)
-            if p < NT:
-                e1(p); eg(p); emu(p)
+                mm2(p); e1(p); eg(p); emu(p)
             if p + 4 < NT:
                 aqz(p + 4)
             if 0 <= p - 1 < NT:
-                eq(p - 1); e4(p - 1)
-                if p % 4 == 0:
-                    er(p // 4 - 1)
-        for it in range(NT):
-            e5(it)
+                eq(p - 1)
+                if p % 2 == 0:
+                    er(p // 2 - 1)
+            if 0 <= p - LAG4 < NT:
+                e4(p - LAG4)
+            if 0 <= p - LAG5 < NT:
+                e5(p - LAG5)

@@ -33,7 +33,8 @@ def tile_gcnlayer_pa_kernel(tc, x, adj, W1, b1, ln_gamma, ln_beta, out):
         keep = ctx.enter_context(tc.tile_pool(name="keep", bufs=1))
         junk = ctx.enter_context(tc.tile_pool(name="junk", bufs=2))
         ps_t = ctx.enter_context(tc.psum_pool(name="ps_t", bufs=5))
-        ps_o = ctx.enter_context(tc.psum_pool(name="ps_o", bufs=3))
+        ps_o = ctx.enter_context(tc.psum_pool(name="ps_o", bufs=2))
+        ps_c = ctx.enter_context(tc.psum_pool(name="ps_c", bufs=1))
 
         vec = keep.tile([P, 3, 512], BF16)
         nc.vector.memset(vec[:], 0.0)
@@ -86,16 +87,22 @@ def tile_gcnlayer_pa_kernel(tc, x, adj, W1, b1, ln_gamma, ln_beta, out):
                 in_=w1g[:, f0 : f0 + fn, :].rearrange("p f t -> p (f t)"),
             )
 
-        vbc = keep.tile([P, 3, F], F32)
+        b1bc = keep.tile([P, F], F32)
+        gb = ps_c.tile([P, 1024], BF16)
         pbs = {}
 
         def bcm(v):
-            pb = ps_o.tile([P, 512], F32, tag="o", name="pb%d" % v)
-            nc.tensor.matmul(out=pb[:], lhsT=ones[:], rhs=vec[:, v, :], start=True, stop=True)
-            pbs[v] = pb
+            if v == 0:
+                pb = ps_o.tile([P, 512], F32, tag="o", name="pb0")
+                nc.tensor.matmul(out=pb[:], lhsT=ones[:], rhs=vec[:, 0, :], start=True, stop=True)
+                pbs[0] = pb
+            else:
+                nc.tensor.matmul(
+                    out=gb[:, 512 * (v - 1) : 512 * v], lhsT=ones[:], rhs=vec[:, v, :], start=True, stop=True
+                )
 
         def bce(v):
-            nc.scalar.copy(out=vbc[:, v, :], in_=pbs[v][:, 0:F])
+            nc.scalar.copy(out=b1bc[:], in_=pbs[v][:, 0:F])
 
         xq = keep.tile([P, N], U32, align_bytes=64)
         xs = keep.tile([P, N], U8, align_bytes=64)
@@ -162,7 +169,7 @@ def tile_gcnlayer_pa_kernel(tc, x, adj, W1, b1, ln_gamma, ln_beta, out):
             phs[jt] = ph
 
         def tp(jt):
-            nc.vector.tensor_tensor(out=T[:, jt, :], in0=phs[jt][:, 0:F], in1=vbc[:, 0, :], op=ALU.add)
+            nc.vector.tensor_tensor(out=T[:, jt, :], in0=phs[jt][:, 0:F], in1=b1bc[:], op=ALU.add)
 
         def aT(it):
             aw = a_sb[it // 2][:].bitcast(F32)
@@ -282,7 +289,7 @@ def tile_gcnlayer_pa_kernel(tc, x, adj, W1, b1, ln_gamma, ln_beta, out):
         def e4(it):
             w = keep.tile([P, F], F32, name="w%d" % it)
             nc.vector.scalar_tensor_tensor(
-                out=w[:], in0=gls[it][:], scalar=negmu[:, it : it + 1], in1=vbc[:, 1, :],
+                out=w[:], in0=gls[it][:], scalar=negmu[:, it : it + 1], in1=gb[:, 0:F],
                 op0=ALU.add, op1=ALU.mult,
             )
             ws[it] = w
@@ -290,7 +297,7 @@ def tile_gcnlayer_pa_kernel(tc, x, adj, W1, b1, ln_gamma, ln_beta, out):
         def e5(it):
             o = keep.tile([P, F], F32, name="o%d" % it)
             nc.vector.scalar_tensor_tensor(
-                out=o[:], in0=ws[it][:], scalar=rstd[:, it : it + 1], in1=vbc[:, 2, :],
+                out=o[:], in0=ws[it][:], scalar=rstd[:, it : it + 1], in1=gb[:, 512 : 512 + F],
                 op0=ALU.mult, op1=ALU.add,
             )
             nc.sync.dma_start(out=out_v[:, it // 2, it % 2, :], in_=o[:])
@@ -305,7 +312,7 @@ def tile_gcnlayer_pa_kernel(tc, x, adj, W1, b1, ln_gamma, ln_beta, out):
         aT(1); aT(2); bcm(1); bcm(2); aT(3); aT(4); aT(5)
         ae(1); ae(2); aT(6); aT(7)
         nc.scalar.activation(out=warm2[:], in_=ones_f[:, 0:1], func=ACT.Gelu)
-        ae(3); bce(1); bce(2); ae(4); ae(5); ae(6); ae(7)
+        ae(3); ae(4); ae(5); ae(6); ae(7)
         drc(0); f2(0); hqz(0); drc(1); f2(1); hqz(1)
         aqz(0); aqz(1); aqz(2); aqz(3)
 

@@ -313,8 +313,8 @@ def tile_gcnlayer_pa_kernel(tc, x, adj, W1, b1, ln_gamma, ln_beta, out):
         ae(1); ae(2); aT(6); aT(7)
         nc.scalar.activation(out=warm2[:], in_=ones_f[:, 0:1], func=ACT.Gelu)
         ae(3); ae(4); ae(5); ae(6); ae(7)
-        drc(0); f2(0); hqz(0); drc(1); f2(1); hqz(1)
-        aqz(0); aqz(1); aqz(2); aqz(3)
+        drc(0); f2(0); aqz(0); hqz(0); drc(1); f2(1); aqz(1); hqz(1)
+        aqz(2); aqz(3)
 
         for p in range(NT + LAG5):
             if p < NT:

@@ -54,10 +54,6 @@ def tile_gcnlayer_pa_kernel(tc, x, adj, W1, b1, ln_gamma, ln_beta, out):
         nc.scalar.activation(out=warm[:], in_=ones_f[:, 0:1], func=ACT.Sqrt)
 
         w1_sb = keep.tile([P, 4, F], BF16)
-        nc.sync.dma_start(
-            out=w1_sb[:].rearrange("p (u e) f -> p u e f", u=2),
-            in_=W1.rearrange("(u p e) f -> p u e f", u=2, e=2),
-        )
         x_sb = []
         for c in range(NCH):
             xt = keep.tile([P, 2 * K], BF16, name="x_sb%d" % c)
@@ -66,6 +62,11 @@ def tile_gcnlayer_pa_kernel(tc, x, adj, W1, b1, ln_gamma, ln_beta, out):
                 in_=x[256 * c : 256 * (c + 1), :].rearrange("(p e) k -> p e k", e=2),
             )
             x_sb.append(xt)
+            if c == 0:
+                nc.sync.dma_start(
+                    out=w1_sb[:].rearrange("p (u e) f -> p u e f", u=2),
+                    in_=W1.rearrange("(u p e) f -> p u e f", u=2, e=2),
+                )
         a_sb = []
         for c in range(NCH):
             at = keep.tile([P, 2, APITCH], BF16, name="a_sb%d" % c)
@@ -77,15 +78,19 @@ def tile_gcnlayer_pa_kernel(tc, x, adj, W1, b1, ln_gamma, ln_beta, out):
             a_sb.append(at)
 
         w1g = keep.tile([P, F, 4], BF16, align_bytes=64)
-        nc.vector.tensor_copy(out=w1g[:], in_=w1_sb[:].rearrange("p t f -> p f t"))
         w1q = keep.tile([P, F], U32, align_bytes=64)
         w1s = keep.tile([P, F], U8, align_bytes=64)
-        for f0, fn in FSPLIT:
-            nc.vector.quantize_mx(
-                out=w1q[:, f0 : f0 + fn].bitcast(FP8X4),
-                scales=w1s[:, f0 : f0 + fn],
-                in_=w1g[:, f0 : f0 + fn, :].rearrange("p f t -> p (f t)"),
-            )
+
+        def w1regroup():
+            nc.vector.tensor_copy(out=w1g[:], in_=w1_sb[:].rearrange("p t f -> p f t"))
+
+        def w1qz():
+            for f0, fn in FSPLIT:
+                nc.vector.quantize_mx(
+                    out=w1q[:, f0 : f0 + fn].bitcast(FP8X4),
+                    scales=w1s[:, f0 : f0 + fn],
+                    in_=w1g[:, f0 : f0 + fn, :].rearrange("p f t -> p (f t)"),
+                )
 
         b1bc = keep.tile([P, F], F32)
         gb = ps_c.tile([P, 1024], BF16)
@@ -303,17 +308,17 @@ def tile_gcnlayer_pa_kernel(tc, x, adj, W1, b1, ln_gamma, ln_beta, out):
             nc.sync.dma_start(out=out_v[:, it // 2, it % 2, :], in_=o[:])
 
         xT(0); xT(1); xe(0); xe(1); bcm(0); bce(0); xT(2); xT(3); xe(2); xe(3)
-        xqz(0); xqz(1); mm1(0); mm1(1); mm1(2); mm1(3)
+        w1regroup(); xqz(0); w1qz(); xqz(1); mm1(0); mm1(1); mm1(2); mm1(3)
         deg(1); xqz(2); tp(0); xqz(3); tp(1)
         aT(0); mm1(4); mm1(5); mm1(6); mm1(7)
         deg(0); deg(2); deg(3); dsq(0)
-        tp(2); tp(3); tp(4); tp(5); deg(5); tp(6); tp(7); deg(7)
-        ae(0); deg(4); deg(6); dsq(1)
+        tp(2); tp(3); tp(4); tp(5); deg(5); tp(6); drc(0); tp(7); deg(7)
+        ae(0); deg(4); deg(6)
         aT(1); aT(2); bcm(1); bcm(2); aT(3); aT(4); aT(5)
-        ae(1); ae(2); aT(6); aT(7)
+        ae(1); dsq(1); ae(2); aT(6); aT(7)
         nc.scalar.activation(out=warm2[:], in_=ones_f[:, 0:1], func=ACT.Gelu)
         ae(3); ae(4); ae(5); ae(6); ae(7)
-        drc(0); f2(0); aqz(0); hqz(0); drc(1); f2(1); aqz(1); hqz(1)
+        f2(0); drc(1); aqz(0); hqz(0); f2(1); aqz(1); hqz(1)
         aqz(2); aqz(3)
 
         for p in range(NT + LAG5):

@@ -20,8 +20,8 @@ NCH = 4
 NT = 8
 APITCH = 1040
 FSPLIT = ((0, 256), (256, 128))
-LAG4 = 3
-LAG5 = 5
+LAG4 = 4
+LAG5 = 6
 
 FLOPS = 2 * N * K * F + 2 * N * N * F
 
@@ -307,15 +307,15 @@ def tile_gcnlayer_pa_kernel(tc, x, adj, W1, b1, ln_gamma, ln_beta, out):
             )
             nc.sync.dma_start(out=out_v[:, it // 2, it % 2, :], in_=o[:])
 
-        xT(0); xT(1); xe(0); xe(1); bcm(0); bce(0); xT(2); xT(3); xe(2); xe(3)
+        xT(0); xT(1); xe(0); xe(1); xT(2); xe(2); bcm(0); bce(0); xT(3); xe(3)
         w1regroup(); xqz(0); w1qz(); xqz(1); mm1(0); mm1(1); mm1(2); mm1(3)
         deg(1); xqz(2); tp(0); xqz(3); tp(1)
         aT(0); mm1(4); mm1(5); mm1(6); mm1(7)
         deg(0); deg(2); deg(3); dsq(0)
         tp(2); tp(3); tp(4); tp(5); deg(5); tp(6); drc(0); tp(7); deg(7)
         ae(0); deg(4); deg(6)
-        aT(1); aT(2); bcm(1); bcm(2); aT(3); aT(4); aT(5)
-        ae(1); dsq(1); ae(2); aT(6); aT(7)
+        aT(1); aT(2); aT(3); aT(4); aT(5)
+        ae(1); dsq(1); ae(2); aT(6); aT(7); bcm(1); bcm(2)
         nc.scalar.activation(out=warm2[:], in_=ones_f[:, 0:1], func=ACT.Gelu)
         ae(3); ae(4); ae(5); ae(6); ae(7)
         f2(0); drc(1); aqz(0); hqz(0); f2(1); aqz(1); hqz(1)

@@ -82,7 +82,9 @@ def tile_gcnlayer_pa_kernel(tc, x, adj, W1, b1, ln_gamma, ln_beta, out):
         w1s = keep.tile([P, F], U8, align_bytes=64)
 
         def w1regroup():
-            nc.vector.tensor_copy(out=w1g[:], in_=w1_sb[:].rearrange("p t f -> p f t"))
+            nc.vector.tensor_copy(
+                out=w1g[:].rearrange("p (c i) t -> p c t i", i=4), in_=w1_sb[:].rearrange("p t (c i) -> p c t i", i=4)
+            )
 
         def w1qz():
             for f0, fn in FSPLIT:
@@ -224,9 +226,9 @@ def tile_gcnlayer_pa_kernel(tc, x, adj, W1, b1, ln_gamma, ln_beta, out):
         def f2(g):
             hsb = keep.tile([P, F, 4], BF16, align_bytes=64, name="hsb%d" % g)
             nc.vector.tensor_tensor(
-                out=hsb[:],
-                in0=T[:, 4 * g : 4 * g + 4, :].rearrange("p t f -> p f t"),
-                in1=dinv[:, 4 * g : 4 * g + 4].unsqueeze(1).to_broadcast([P, F, 4]),
+                out=hsb[:].rearrange("p (c i) t -> p c t i", i=4),
+                in0=T[:, 4 * g : 4 * g + 4, :].rearrange("p t (c i) -> p c t i", i=4),
+                in1=dinv[:, 4 * g : 4 * g + 4].unsqueeze(1).unsqueeze(3).to_broadcast([P, F // 4, 4, 4]),
                 op=ALU.mult,
             )
             hsbs[g] = hsb

@@ -233,6 +233,21 @@ def tile_gcnlayer_pa_kernel(tc, x, adj, W1, b1, ln_gamma, ln_beta, out):
             )
             hsbs[g] = hsb
 
+        hnat = keep.tile([P, 4, F], BF16)
+
+        def hg(jt):
+            nc.gpsimd.tensor_scalar(
+                out=hnat[:, jt, :], in0=T[:, jt, :], scalar1=dinv[:, jt : jt + 1], scalar2=0.0,
+                op0=ALU.mult, op1=ALU.add,
+            )
+
+        def il():
+            hsb = keep.tile([P, F, 4], BF16, align_bytes=64, name="hsb0")
+            nc.vector.tensor_copy(
+                out=hsb[:].rearrange("p (c i) t -> p c t i", i=4), in_=hnat[:].rearrange("p t (c i) -> p c t i", i=4)
+            )
+            hsbs[0] = hsb
+
         def hqz(g):
             for f0, fn in FSPLIT:
                 nc.vector.quantize_mx(
@@ -314,13 +329,14 @@ def tile_gcnlayer_pa_kernel(tc, x, adj, W1, b1, ln_gamma, ln_beta, out):
         deg(1); xqz(2); tp(0); xqz(3); tp(1)
         aT(0); mm1(4); mm1(5); mm1(6); mm1(7)
         deg(0); deg(2); deg(3); dsq(0)
-        tp(2); tp(3); tp(4); tp(5); deg(5); tp(6); drc(0); tp(7); deg(7)
+        tp(2); tp(3); drc(0); hg(0); hg(1); hg(2); hg(3)
+        tp(4); tp(5); deg(5); tp(6); tp(7); deg(7)
         ae(0); deg(4); deg(6)
         aT(1); aT(2); aT(3); aT(4); aT(5)
         ae(1); dsq(1); ae(2); aT(6); aT(7); bcm(1); bcm(2)
         nc.scalar.activation(out=warm2[:], in_=ones_f[:, 0:1], func=ACT.Gelu)
         ae(3); ae(4); ae(5); ae(6); ae(7)
-        f2(0); drc(1); aqz(0); hqz(0); f2(1); aqz(1); hqz(1)
+        il(); drc(1); aqz(0); hqz(0); f2(1); aqz(1); hqz(1)
         aqz(2); aqz(3)
 
         for p in range(NT + LAG5):

@@ -36,12 +36,14 @@ def tile_gcnlayer_pa_kernel(tc, x, adj, W1, b1, ln_gamma, ln_beta, out):
         ps_o = ctx.enter_context(tc.psum_pool(name="ps_o", bufs=2))
         ps_c = ctx.enter_context(tc.psum_pool(name="ps_c", bufs=1))
 
+        ones_f = keep.tile([P, 1], F32)
+        nc.vector.memset(ones_f[:], 1.0)
+        warm = keep.tile([P, 1], F32)
+        nc.scalar.activation(out=warm[:], in_=ones_f[:], func=ACT.Sqrt)
         vec = keep.tile([P, 3, 512], BF16)
         nc.vector.memset(vec[:], 0.0)
         neghalf = keep.tile([P, 4], F32)
         nc.vector.memset(neghalf[:], -0.5)
-        ones_f = keep.tile([P, 1], F32)
-        nc.vector.memset(ones_f[:], 1.0)
         ones = keep.tile([P, P], BF16)
         nc.vector.memset(ones[:], 1.0)
         ident = keep.tile([P, P], F32)
@@ -50,41 +52,54 @@ def tile_gcnlayer_pa_kernel(tc, x, adj, W1, b1, ln_gamma, ln_beta, out):
         nc.scalar.dma_start(out=vec[0:1, 0, 0:F], in_=b1.unsqueeze(0))
         nc.scalar.dma_start(out=vec[0:1, 1, 0:F], in_=ln_gamma.unsqueeze(0))
         nc.scalar.dma_start(out=vec[0:1, 2, 0:F], in_=ln_beta.unsqueeze(0))
-        warm = keep.tile([P, 1], F32)
-        nc.scalar.activation(out=warm[:], in_=ones_f[:, 0:1], func=ACT.Sqrt)
 
         w1_sb = keep.tile([P, 4, F], BF16)
-        x_sb = []
+        x_sb = [keep.tile([P, 2 * K], BF16, name="x_sb%d" % c) for c in range(NCH)]
+        a_sb = [keep.tile([P, 2, APITCH], BF16, name="a_sb%d" % c) for c in range(NCH)]
         for c in range(NCH):
-            xt = keep.tile([P, 2 * K], BF16, name="x_sb%d" % c)
+            nc.vector.memset(a_sb[c][:, :, N : N + 1], 1.0)
+
+        def lw():
             nc.sync.dma_start(
-                out=xt[:].rearrange("p (e k) -> p e k", e=2),
+                out=w1_sb[:].rearrange("p (u e) f -> p u e f", u=2),
+                in_=W1.rearrange("(u p e) f -> p u e f", u=2, e=2),
+            )
+
+        def lx(c):
+            nc.sync.dma_start(
+                out=x_sb[c][:].rearrange("p (e k) -> p e k", e=2),
                 in_=x[256 * c : 256 * (c + 1), :].rearrange("(p e) k -> p e k", e=2),
             )
-            x_sb.append(xt)
-            if c == 0:
-                nc.sync.dma_start(
-                    out=w1_sb[:].rearrange("p (u e) f -> p u e f", u=2),
-                    in_=W1.rearrange("(u p e) f -> p u e f", u=2, e=2),
-                )
-        a_sb = []
-        for c in range(NCH):
-            at = keep.tile([P, 2, APITCH], BF16, name="a_sb%d" % c)
-            nc.vector.memset(at[:, :, N : N + 1], 1.0)
+
+        def la(c):
             nc.sync.dma_start(
-                out=at[:, :, 0:N],
+                out=a_sb[c][:, :, 0:N],
                 in_=adj[256 * c : 256 * (c + 1), :].rearrange("(p e) j -> p e j", e=2),
             )
-            a_sb.append(at)
+
+        def lah(c, e):
+            nc.sync.dma_start(
+                out=a_sb[c][:, e, 0:N],
+                in_=adj[256 * c : 256 * (c + 1), :].rearrange("(p e) j -> p e j", e=2)[:, e, :],
+            )
+
+        lx(0); lw(); lx(1); lx(2); lah(0, 1); lx(3); lah(0, 0); la(1); la(2); la(3)
 
         w1g = keep.tile([P, F, 4], BF16, align_bytes=64)
         w1q = keep.tile([P, F], U32, align_bytes=64)
         w1s = keep.tile([P, F], U8, align_bytes=64)
 
-        def w1regroup():
-            nc.vector.tensor_copy(
-                out=w1g[:].rearrange("p (c i) t -> p c t i", i=4), in_=w1_sb[:].rearrange("p t (c i) -> p c t i", i=4)
+        def interleave(copy, dst, src, f0, fn):
+            copy(
+                out=dst[:, f0 : f0 + fn, :].rearrange("p (c i) t -> p c t i", i=4),
+                in_=src[:, :, f0 : f0 + fn].rearrange("p t (c i) -> p c t i", i=4),
             )
+
+        def w1v(f0=0, fn=F):
+            interleave(nc.vector.tensor_copy, w1g, w1_sb, f0, fn)
+
+        def w1s_(f0, fn):
+            interleave(nc.scalar.copy, w1g, w1_sb, f0, fn)
 
         def w1qz():
             for f0, fn in FSPLIT:
@@ -324,8 +339,8 @@ def tile_gcnlayer_pa_kernel(tc, x, adj, W1, b1, ln_gamma, ln_beta, out):
             )
             nc.sync.dma_start(out=out_v[:, it // 2, it % 2, :], in_=o[:])
 
-        xT(0); xT(1); xe(0); xe(1); xT(2); xe(2); bcm(0); bce(0); xT(3); xe(3)
-        w1regroup(); xqz(0); w1qz(); xqz(1); mm1(0); mm1(1); mm1(2); mm1(3)
+        xT(0); xT(1); xe(0); w1s_(256, 128); xe(1); xT(2); xe(2); bcm(0); bce(0); xT(3); xe(3)
+        w1v(0, 256); xqz(0); w1qz(); xqz(1); mm1(0); mm1(1); mm1(2); mm1(3)
         deg(1); xqz(2); tp(0); xqz(3); tp(1)
         aT(0); mm1(4); mm1(5); mm1(6); mm1(7)
         deg(0); deg(2); deg(3); dsq(0)
@@ -338,6 +353,7 @@ def tile_gcnlayer_pa_kernel(tc, x, adj, W1, b1, ln_gamma, ln_beta, out):
         ae(3); ae(4); ae(5); ae(6); ae(7)
         il(); drc(1); aqz(0); hqz(0); f2(1); aqz(1); hqz(1)
         aqz(2); aqz(3)
+
 
         for p in range(NT + LAG5):
             if p < NT:

@@ -39,7 +39,7 @@ def tile_gcnlayer_pa_kernel(tc, x, adj, W1, b1, ln_gamma, ln_beta, out):
         ones_f = keep.tile([P, 1], F32)
         nc.vector.memset(ones_f[:], 1.0)
         warm = keep.tile([P, 1], F32)
-        nc.scalar.activation(out=warm[:], in_=ones_f[:], func=ACT.Sqrt)
+        nc.scalar.activation(out=warm[:], in_=ones_f[:], func=ACT.Abs_reciprocal_sqrt)
         vec = keep.tile([P, 3, 512], BF16)
         nc.vector.memset(vec[:], 0.0)
         neghalf = keep.tile([P, 4], F32)
@@ -133,9 +133,6 @@ def tile_gcnlayer_pa_kernel(tc, x, adj, W1, b1, ln_gamma, ln_beta, out):
         asc = keep.tile([P, 2 * N], U8, align_bytes=64)
         hq = keep.tile([P, 2 * F], U32, align_bytes=64)
         hsc = keep.tile([P, 2 * F], U8, align_bytes=64)
-        deg_s = [keep.tile([P, 2], F32, name="deg_s%d" % g) for g in range(2)]
-        deg_v = [keep.tile([P, 2], F32, name="deg_v%d" % g) for g in range(2)]
-        sdeg = keep.tile([P, NCH, 2], F32)
         warm2 = keep.tile([P, 1], F32)
         dinv = keep.tile([P, NT], F32)
         sumg = keep.tile([P, NT], F32)
@@ -215,28 +212,23 @@ def tile_gcnlayer_pa_kernel(tc, x, adj, W1, b1, ln_gamma, ln_beta, out):
                 in_=ags[it][:],
             )
 
-        def deg(it):
-            c, e = it // 2, it % 2
-            if e == 1:
-                jv = junk.tile([P, N], BF16, tag="jv", name="jv%d" % it)
-                nc.vector.tensor_scalar(
-                    out=jv[:], in0=a_sb[c][:, e, 0:N], scalar1=1.0, scalar2=1.0,
-                    op0=ALU.mult, op1=ALU.add, accum_out=deg_v[c // 2][:, c % 2 : c % 2 + 1],
-                )
-            else:
-                js = junk.tile([P, N + 1], BF16, tag="js", name="js%d" % it)
-                nc.scalar.activation(
-                    out=js[:], in_=a_sb[c][:, e, 0 : N + 1], func=ACT.Copy, accum_out=deg_s[c // 2][:, c % 2 : c % 2 + 1],
-                )
+        dega = keep.tile([P, NT], F32)
 
-        def dsq(g):
-            nc.scalar.activation(out=sdeg[:, 2 * g : 2 * g + 2, 0], in_=deg_s[g][:], func=ACT.Sqrt)
-            nc.scalar.activation(out=sdeg[:, 2 * g : 2 * g + 2, 1], in_=deg_v[g][:], func=ACT.Sqrt)
-
-        def drc(g):
-            nc.vector.reciprocal(
-                out=dinv[:, 4 * g : 4 * g + 4], in_=sdeg[:, 2 * g : 2 * g + 2, :].rearrange("p c e -> p (c e)")
+        def degv(it):
+            jv = junk.tile([P, N], BF16, tag="jv", name="jv%d" % it)
+            nc.vector.tensor_scalar(
+                out=jv[:], in0=a_sb[it // 2][:, it % 2, 0:N], scalar1=1.0, scalar2=1.0,
+                op0=ALU.mult, op1=ALU.add, accum_out=dega[:, it : it + 1],
             )
+
+        def degs(it):
+            js = junk.tile([P, N + 1], BF16, tag="js", name="js%d" % it)
+            nc.scalar.activation(
+                out=js[:], in_=a_sb[it // 2][:, it % 2, 0 : N + 1], func=ACT.Copy, accum_out=dega[:, it : it + 1],
+            )
+
+        def drs(g):
+            nc.scalar.activation(out=dinv[:, 4 * g : 4 * g + 4], in_=dega[:, 4 * g : 4 * g + 4], func=ACT.Abs_reciprocal_sqrt)
 
         def f2(g):
             hsb = keep.tile([P, F, 4], BF16, align_bytes=64, name="hsb%d" % g)
@@ -247,6 +239,12 @@ def tile_gcnlayer_pa_kernel(tc, x, adj, W1, b1, ln_gamma, ln_beta, out):
                 op=ALU.mult,
             )
             hsbs[g] = hsb
+
+        def hv(jt):
+            nc.vector.tensor_scalar(
+                out=hnat[:, jt, :], in0=T[:, jt, :], scalar1=dinv[:, jt : jt + 1], scalar2=0.0,
+                op0=ALU.mult, op1=ALU.add,
+            )
 
         hnat = keep.tile([P, 4, F], BF16)
 
@@ -341,17 +339,17 @@ def tile_gcnlayer_pa_kernel(tc, x, adj, W1, b1, ln_gamma, ln_beta, out):
 
         xT(0); xT(1); xe(0); w1s_(256, 128); xe(1); xT(2); xe(2); bcm(0); bce(0); xT(3); xe(3)
         w1v(0, 256); xqz(0); w1qz(); xqz(1); mm1(0); mm1(1); mm1(2); mm1(3)
-        deg(1); xqz(2); tp(0); xqz(3); tp(1)
+        degv(1); xqz(2); tp(0); xqz(3); tp(1)
         aT(0); mm1(4); mm1(5); mm1(6); mm1(7)
-        deg(0); deg(2); deg(3); dsq(0)
-        tp(2); tp(3); drc(0); hg(0); hg(1); hg(2); hg(3)
-        tp(4); tp(5); deg(5); tp(6); tp(7); deg(7)
-        ae(0); deg(4); deg(6)
+        degs(0); degs(2); degv(3); drs(0)
+        tp(2); tp(3); hg(0); hg(1); hg(2); hg(3)
+        tp(4); tp(5); degv(5); tp(6); tp(7); degv(7)
+        ae(0); degs(4); degs(6)
         aT(1); aT(2); aT(3); aT(4); aT(5)
-        ae(1); dsq(1); ae(2); aT(6); aT(7); bcm(1); bcm(2)
+        ae(1); drs(1); ae(2); aT(6); aT(7); bcm(1); bcm(2)
         nc.scalar.activation(out=warm2[:], in_=ones_f[:, 0:1], func=ACT.Gelu)
         ae(3); ae(4); ae(5); ae(6); ae(7)
-        il(); drc(1); aqz(0); hqz(0); f2(1); aqz(1); hqz(1)
+        il(); aqz(0); hqz(0); f2(1); aqz(1); hqz(1)
         aqz(2); aqz(3)
 
 

@@ -36,22 +36,20 @@ def tile_gcnlayer_pa_kernel(tc, x, adj, W1, b1, ln_gamma, ln_beta, out):
         ps_o = ctx.enter_context(tc.psum_pool(name="ps_o", bufs=2))
         ps_c = ctx.enter_context(tc.psum_pool(name="ps_c", bufs=1))
 
+        vec = keep.tile([P, 3, 512], BF16)
+        nc.vector.memset(vec[:, 0, :], 0.0)
+        nc.scalar.dma_start(out=vec[0:1, 0, 0:F], in_=b1.unsqueeze(0))
         ones_f = keep.tile([P, 1], F32)
         nc.vector.memset(ones_f[:], 1.0)
         warm = keep.tile([P, 1], F32)
         nc.scalar.activation(out=warm[:], in_=ones_f[:], func=ACT.Abs_reciprocal_sqrt)
-        vec = keep.tile([P, 3, 512], BF16)
-        nc.vector.memset(vec[:], 0.0)
+        nc.vector.memset(vec[:, 1:3, :], 0.0)
         neghalf = keep.tile([P, 4], F32)
         nc.vector.memset(neghalf[:], -0.5)
         ones = keep.tile([P, P], BF16)
         nc.vector.memset(ones[:], 1.0)
         ident = keep.tile([P, P], F32)
         make_identity(nc, ident[:])
-
-        nc.scalar.dma_start(out=vec[0:1, 0, 0:F], in_=b1.unsqueeze(0))
-        nc.scalar.dma_start(out=vec[0:1, 1, 0:F], in_=ln_gamma.unsqueeze(0))
-        nc.scalar.dma_start(out=vec[0:1, 2, 0:F], in_=ln_beta.unsqueeze(0))
 
         w1_sb = keep.tile([P, 4, F], BF16)
         x_sb = [keep.tile([P, 2 * K], BF16, name="x_sb%d" % c) for c in range(NCH)]
@@ -84,6 +82,8 @@ def tile_gcnlayer_pa_kernel(tc, x, adj, W1, b1, ln_gamma, ln_beta, out):
             )
 
         lx(0); lw(); lx(1); lx(2); lah(0, 1); lx(3); lah(0, 0); la(1); la(2); la(3)
+        nc.sync.dma_start(out=vec[0:1, 1, 0:F], in_=ln_gamma.unsqueeze(0))
+        nc.sync.dma_start(out=vec[0:1, 2, 0:F], in_=ln_beta.unsqueeze(0))
 
         w1g = keep.tile([P, F, 4], BF16, align_bytes=64)
         w1q = keep.tile([P, F], U32, align_bytes=64)

@@ -18,7 +18,6 @@ F = 384
 EPS = 1e-6
 NCH = 4
 NT = 8
-APITCH = 1040
 FSPLIT = ((0, 256), (256, 128))
 LAG4 = 4
 LAG5 = 6
@@ -53,9 +52,7 @@ def tile_gcnlayer_pa_kernel(tc, x, adj, W1, b1, ln_gamma, ln_beta, out):
 
         w1_sb = keep.tile([P, 4, F], BF16)
         x_sb = [keep.tile([P, 2 * K], BF16, name="x_sb%d" % c) for c in range(NCH)]
-        a_sb = [keep.tile([P, 2, APITCH], BF16, name="a_sb%d" % c) for c in range(NCH)]
-        for c in range(NCH):
-            nc.vector.memset(a_sb[c][:, :, N : N + 1], 1.0)
+        a_sb = [keep.tile([P, 2, N], BF16, name="a_sb%d" % c) for c in range(NCH)]
 
         def lw():
             nc.sync.dma_start(
@@ -71,19 +68,16 @@ def tile_gcnlayer_pa_kernel(tc, x, adj, W1, b1, ln_gamma, ln_beta, out):
 
         def la(c):
             nc.sync.dma_start(
-                out=a_sb[c][:, :, 0:N],
+                out=a_sb[c][:],
                 in_=adj[256 * c : 256 * (c + 1), :].rearrange("(p e) j -> p e j", e=2),
             )
 
         def lah(c, e):
             nc.sync.dma_start(
-                out=a_sb[c][:, e, 0:N],
+                out=a_sb[c][:, e, :],
                 in_=adj[256 * c : 256 * (c + 1), :].rearrange("(p e) j -> p e j", e=2)[:, e, :],
             )
 
-        lx(0); lw(); lx(1); lx(2); lah(0, 1); lx(3); lah(0, 0); la(1); la(2); la(3)
-        nc.sync.dma_start(out=vec[0:1, 1, 0:F], in_=ln_gamma.unsqueeze(0))
-        nc.sync.dma_start(out=vec[0:1, 2, 0:F], in_=ln_beta.unsqueeze(0))
 
         w1g = keep.tile([P, F, 4], BF16, align_bytes=64)
         w1q = keep.tile([P, F], U32, align_bytes=64)
@@ -217,18 +211,18 @@ def tile_gcnlayer_pa_kernel(tc, x, adj, W1, b1, ln_gamma, ln_beta, out):
         def degv(it):
             jv = junk.tile([P, N], BF16, tag="jv", name="jv%d" % it)
             nc.vector.tensor_scalar(
-                out=jv[:], in0=a_sb[it // 2][:, it % 2, 0:N], scalar1=1.0, scalar2=1.0,
+                out=jv[:], in0=a_sb[it // 2][:, it % 2, :], scalar1=1.0, scalar2=0.0,
                 op0=ALU.mult, op1=ALU.add, accum_out=dega[:, it : it + 1],
             )
 
         def degs(it):
-            js = junk.tile([P, N + 1], BF16, tag="js", name="js%d" % it)
+            js = junk.tile([P, N], BF16, tag="js", name="js%d" % it)
             nc.scalar.activation(
-                out=js[:], in_=a_sb[it // 2][:, it % 2, 0 : N + 1], func=ACT.Copy, accum_out=dega[:, it : it + 1],
+                out=js[:], in_=a_sb[it // 2][:, it % 2, :], func=ACT.Copy, accum_out=dega[:, it : it + 1],
             )
 
         def drs(g):
-            nc.scalar.activation(out=dinv[:, 4 * g : 4 * g + 4], in_=dega[:, 4 * g : 4 * g + 4], func=ACT.Abs_reciprocal_sqrt)
+            nc.scalar.activation(out=dinv[:, 4 * g : 4 * g + 4], in_=dega[:, 4 * g : 4 * g + 4], func=ACT.Abs_reciprocal_sqrt, bias=1.0)
 
         def f2(g):
             hsb = keep.tile([P, F, 4], BF16, align_bytes=64, name="hsb%d" % g)
@@ -337,6 +331,10 @@ def tile_gcnlayer_pa_kernel(tc, x, adj, W1, b1, ln_gamma, ln_beta, out):
             )
             nc.sync.dma_start(out=out_v[:, it // 2, it % 2, :], in_=o[:])
 
+        def lg(v):
+            nc.sync.dma_start(out=vec[0:1, v, 0:F], in_=(ln_gamma if v == 1 else ln_beta).unsqueeze(0))
+
+        lx(0); lw(); lx(1); lx(2); lah(0, 1); lx(3); lah(0, 0); la(1); la(2); la(3); lg(1); lg(2)
         xT(0); xT(1); xe(0); w1s_(256, 128); xe(1); xT(2); xe(2); bcm(0); bce(0); xT(3); xe(3)
         w1v(0, 256); xqz(0); w1qz(); xqz(1); mm1(0); mm1(1); mm1(2); mm1(3)
         degv(1); xqz(2); tp(0); xqz(3); tp(1)

@@ -103,13 +103,13 @@ def tile_gcnlayer_pa_kernel(tc, x, adj, W1, b1, ln_gamma, ln_beta, out):
                     in_=w1g[:, f0 : f0 + fn, :].rearrange("p f t -> p (f t)"),
                 )
 
-        b1bc = keep.tile([P, F], F32)
+        b1bc = keep.tile([P, F], BF16)
         gb = ps_c.tile([P, 1024], BF16)
         pbs = {}
 
         def bcm(v):
             if v == 0:
-                pb = ps_o.tile([P, 512], F32, tag="o", name="pb0")
+                pb = ps_o.tile([P, 512], BF16, tag="o", name="pb0")
                 nc.tensor.matmul(out=pb[:], lhsT=ones[:], rhs=vec[:, 0, :], start=True, stop=True)
                 pbs[0] = pb
             else:
@@ -331,6 +331,15 @@ def tile_gcnlayer_pa_kernel(tc, x, adj, W1, b1, ln_gamma, ln_beta, out):
             )
             nc.sync.dma_start(out=out_v[:, it // 2, it % 2, :], in_=o[:])
 
+        def e5s(it):
+            for f0, fn in FSPLIT:
+                o = keep.tile([P, fn], F32, name="o%d_%d" % (it, f0))
+                nc.vector.scalar_tensor_tensor(
+                    out=o[:], in0=ws[it][:, f0 : f0 + fn], scalar=rstd[:, it : it + 1], in1=gb[:, 512 + f0 : 512 + f0 + fn],
+                    op0=ALU.mult, op1=ALU.add,
+                )
+                nc.sync.dma_start(out=out_v[:, it // 2, it % 2, f0 : f0 + fn], in_=o[:])
+
         def lg(v):
             nc.sync.dma_start(out=vec[0:1, v, 0:F], in_=(ln_gamma if v == 1 else ln_beta).unsqueeze(0))
 
@@ -362,5 +371,6 @@ def tile_gcnlayer_pa_kernel(tc, x, adj, W1, b1, ln_gamma, ln_beta, out):
                     er(p // 2 - 1)
             if 0 <= p - LAG4 < NT:
                 e4(p - LAG4)
-            if 0 <= p - LAG5 < NT:
+            if 0 <= p - LAG5 < NT - 1:
                 e5(p - LAG5)
+        e5s(NT - 1)

from contextlib import ExitStack

import concourse.mybir as mybir
from concourse.masks import make_identity

F32 = mybir.dt.float32
BF16 = mybir.dt.bfloat16
U32 = mybir.dt.uint32
U8 = mybir.dt.uint8
FP8X4 = mybir.dt.float8_e4m3fn_x4
ALU = mybir.AluOpType
ACT = mybir.ActivationFunctionType

P = 128
N = 1024
K = 512
F = 384
EPS = 1e-6
NCH = 4
NT = 8
FSPLIT = ((0, 256), (256, 128))
LAG4 = 4
LAG5 = 6

FLOPS = 2 * N * K * F + 2 * N * N * F


def tile_gcnlayer_pa_kernel(tc, x, adj, W1, b1, ln_gamma, ln_beta, out):
    nc = tc.nc
    with ExitStack() as ctx:
        ctx.enter_context(tc.manual_schedule())
        keep = ctx.enter_context(tc.tile_pool(name="keep", bufs=1))
        junk = ctx.enter_context(tc.tile_pool(name="junk", bufs=2))
        ps_t = ctx.enter_context(tc.psum_pool(name="ps_t", bufs=5))
        ps_o = ctx.enter_context(tc.psum_pool(name="ps_o", bufs=2))
        ps_c = ctx.enter_context(tc.psum_pool(name="ps_c", bufs=1))

        vec = keep.tile([P, 3, 512], BF16)
        nc.vector.memset(vec[:, 0, :], 0.0)
        nc.scalar.dma_start(out=vec[0:1, 0, 0:F], in_=b1.unsqueeze(0))
        ones_f = keep.tile([P, 1], F32)
        nc.vector.memset(ones_f[:], 1.0)
        warm = keep.tile([P, 1], F32)
        nc.scalar.activation(out=warm[:], in_=ones_f[:], func=ACT.Abs_reciprocal_sqrt)
        nc.vector.memset(vec[:, 1:3, :], 0.0)
        neghalf = keep.tile([P, 4], F32)
        nc.vector.memset(neghalf[:], -0.5)
        ones = keep.tile([P, P], BF16)
        nc.vector.memset(ones[:], 1.0)
        ident = keep.tile([P, P], F32)
        make_identity(nc, ident[:])

        w1_sb = keep.tile([P, 4, F], BF16)
        x_sb = [keep.tile([P, 2 * K], BF16, name="x_sb%d" % c) for c in range(NCH)]
        a_sb = [keep.tile([P, 2, N], BF16, name="a_sb%d" % c) for c in range(NCH)]

        def lw():
            nc.sync.dma_start(
                out=w1_sb[:].rearrange("p (u e) f -> p u e f", u=2),
                in_=W1.rearrange("(u p e) f -> p u e f", u=2, e=2),
            )

        def lx(c):
            nc.sync.dma_start(
                out=x_sb[c][:].rearrange("p (e k) -> p e k", e=2),
                in_=x[256 * c : 256 * (c + 1), :].rearrange("(p e) k -> p e k", e=2),
            )

        def la(c):
            nc.sync.dma_start(
                out=a_sb[c][:],
                in_=adj[256 * c : 256 * (c + 1), :].rearrange("(p e) j -> p e j", e=2),
            )

        def lah(c, e):
            nc.sync.dma_start(
                out=a_sb[c][:, e, :],
                in_=adj[256 * c : 256 * (c + 1), :].rearrange("(p e) j -> p e j", e=2)[:, e, :],
            )


        w1g = keep.tile([P, F, 4], BF16, align_bytes=64)
        w1q = keep.tile([P, F], U32, align_bytes=64)
        w1s = keep.tile([P, F], U8, align_bytes=64)

        def interleave(copy, dst, src, f0, fn):
            copy(
                out=dst[:, f0 : f0 + fn, :].rearrange("p (c i) t -> p c t i", i=4),
                in_=src[:, :, f0 : f0 + fn].rearrange("p t (c i) -> p c t i", i=4),
            )

        def w1v(f0=0, fn=F):
            interleave(nc.vector.tensor_copy, w1g, w1_sb, f0, fn)

        def w1s_(f0, fn):
            interleave(nc.scalar.copy, w1g, w1_sb, f0, fn)

        def w1qz():
            for f0, fn in FSPLIT:
                nc.vector.quantize_mx(
                    out=w1q[:, f0 : f0 + fn].bitcast(FP8X4),
                    scales=w1s[:, f0 : f0 + fn],
                    in_=w1g[:, f0 : f0 + fn, :].rearrange("p f t -> p (f t)"),
                )

        b1bc = keep.tile([P, F], BF16)
        gb = ps_c.tile([P, 1024], BF16)
        pbs = {}

        def bcm(v):
            if v == 0:
                pb = ps_o.tile([P, 512], BF16, tag="o", name="pb0")
                nc.tensor.matmul(out=pb[:], lhsT=ones[:], rhs=vec[:, 0, :], start=True, stop=True)
                pbs[0] = pb
            else:
                nc.tensor.matmul(
                    out=gb[:, 512 * (v - 1) : 512 * v], lhsT=ones[:], rhs=vec[:, v, :], start=True, stop=True
                )

        def bce(v):
            nc.scalar.copy(out=b1bc[:], in_=pbs[v][:, 0:F])

        xq = keep.tile([P, N], U32, align_bytes=64)
        xs = keep.tile([P, N], U8, align_bytes=64)
        T = keep.tile([P, NT, F], F32)
        aq = keep.tile([P, 2 * N], U32, align_bytes=64)
        asc = keep.tile([P, 2 * N], U8, align_bytes=64)
        hq = keep.tile([P, 2 * F], U32, align_bytes=64)
        hsc = keep.tile([P, 2 * F], U8, align_bytes=64)
        warm2 = keep.tile([P, 1], F32)
        dinv = keep.tile([P, NT], F32)
        sumg = keep.tile([P, NT], F32)
        ssq = keep.tile([P, NT], F32)
        negmu = keep.tile([P, NT], F32)
        vare = keep.tile([P, NT], F32)
        rstd = keep.tile([P, NT], F32)
        out_v = out.rearrange("(c p e) f -> p c e f", c=NCH, e=2)
        pts = {}
        xgs = {}
        ags = {}
        phs = {}
        hsbs = {}
        pos = {}
        ss = {}
        gls = {}
        ws = {}

        def xT(c):
            xw = x_sb[c][:].bitcast(F32)
            pt = ps_t.tile([P, 512], F32, tag="t", name="ptx%d" % c)
            for b in range(4):
                nc.tensor.transpose(out=pt[:, 128 * b : 128 * (b + 1)], in_=xw[:, 128 * b : 128 * (b + 1)], identity=ident[:])
            pts[("x", c)] = pt

        def xe(c):
            xg = keep.tile([P, 1024], BF16, align_bytes=64, name="xg%d" % c)
            nc.scalar.copy(
                out=xg[:].bitcast(F32).rearrange("p (e j u) -> p e j u", e=2, u=2),
                in_=pts[("x", c)][:].rearrange("p (e u j) -> p e j u", e=2, u=2),
            )
            xgs[c] = xg

        def xqz(c):
            nc.vector.quantize_mx(
                out=xq[:, 256 * c : 256 * (c + 1)].bitcast(FP8X4),
                scales=xs[:, 256 * c : 256 * (c + 1)],
                in_=xgs[c][:],
            )

        def mm1(jt):
            ph = ps_t.tile([P, 512], F32, tag="t", name="ph%d" % jt)
            for f0, fn in FSPLIT:
                nc.tensor.matmul_mx(
                    out=ph[:, f0 : f0 + fn],
                    lhsT=xq[:, 128 * jt : 128 * (jt + 1)].bitcast(FP8X4),
                    lhsT_scale=xs[:, 128 * jt : 128 * (jt + 1)],
                    rhs=w1q[:, f0 : f0 + fn].bitcast(FP8X4),
                    rhs_scale=w1s[:, f0 : f0 + fn],
                    start=True,
                    stop=True,
                )
            phs[jt] = ph

        def tp(jt):
            nc.vector.tensor_tensor(out=T[:, jt, :], in0=phs[jt][:, 0:F], in1=b1bc[:], op=ALU.add)

        def aT(it):
            aw = a_sb[it // 2][:].bitcast(F32)
            pt = ps_t.tile([P, 512], F32, tag="t", name="pta%d" % it)
            for b in range(4):
                nc.tensor.transpose(out=pt[:, 128 * b : 128 * (b + 1)], in_=aw[:, it % 2, 128 * b : 128 * (b + 1)], identity=ident[:])
            pts[("a", it)] = pt

        def ae(it):
            ag = keep.tile([P, 1024], BF16, align_bytes=64, name="ag%d" % it)
            nc.scalar.copy(
                out=ag[:].bitcast(F32).rearrange("p (g i u) -> p g i u", g=2, u=2),
                in_=pts[("a", it)][:].rearrange("p (g u i) -> p g i u", g=2, u=2),
            )
            ags[it] = ag

        def aqz(it):
            nc.vector.quantize_mx(
                out=aq[:, 256 * it : 256 * (it + 1)].bitcast(FP8X4),
                scales=asc[:, 256 * it : 256 * (it + 1)],
                in_=ags[it][:],
            )

        dega = keep.tile([P, NT], F32)

        def degv(it):
            jv = junk.tile([P, N], BF16, tag="jv", name="jv%d" % it)
            nc.vector.tensor_scalar(
                out=jv[:], in0=a_sb[it // 2][:, it % 2, :], scalar1=1.0, scalar2=0.0,
                op0=ALU.mult, op1=ALU.add, accum_out=dega[:, it : it + 1],
            )

        def degs(it):
            js = junk.tile([P, N], BF16, tag="js", name="js%d" % it)
            nc.scalar.activation(
                out=js[:], in_=a_sb[it // 2][:, it % 2, :], func=ACT.Copy, accum_out=dega[:, it : it + 1],
            )

        def drs(g):
            nc.scalar.activation(out=dinv[:, 4 * g : 4 * g + 4], in_=dega[:, 4 * g : 4 * g + 4], func=ACT.Abs_reciprocal_sqrt, bias=1.0)

        def f2(g):
            hsb = keep.tile([P, F, 4], BF16, align_bytes=64, name="hsb%d" % g)
            nc.vector.tensor_tensor(
                out=hsb[:].rearrange("p (c i) t -> p c t i", i=4),
                in0=T[:, 4 * g : 4 * g + 4, :].rearrange("p t (c i) -> p c t i", i=4),
                in1=dinv[:, 4 * g : 4 * g + 4].unsqueeze(1).unsqueeze(3).to_broadcast([P, F // 4, 4, 4]),
                op=ALU.mult,
            )
            hsbs[g] = hsb

        def hv(jt):
            nc.vector.tensor_scalar(
                out=hnat[:, jt, :], in0=T[:, jt, :], scalar1=dinv[:, jt : jt + 1], scalar2=0.0,
                op0=ALU.mult, op1=ALU.add,
            )

        hnat = keep.tile([P, 4, F], BF16)

        def hg(jt):
            nc.gpsimd.tensor_scalar(
                out=hnat[:, jt, :], in0=T[:, jt, :], scalar1=dinv[:, jt : jt + 1], scalar2=0.0,
                op0=ALU.mult, op1=ALU.add,
            )

        def il():
            hsb = keep.tile([P, F, 4], BF16, align_bytes=64, name="hsb0")
            nc.vector.tensor_copy(
                out=hsb[:].rearrange("p (c i) t -> p c t i", i=4), in_=hnat[:].rearrange("p t (c i) -> p c t i", i=4)
            )
            hsbs[0] = hsb

        def hqz(g):
            for f0, fn in FSPLIT:
                nc.vector.quantize_mx(
                    out=hq[:, F * g + f0 : F * g + f0 + fn].bitcast(FP8X4),
                    scales=hsc[:, F * g + f0 : F * g + f0 + fn],
                    in_=hsbs[g][:, f0 : f0 + fn, :].rearrange("p f t -> p (f t)"),
                )

        def mm2(it):
            po = ps_o.tile([P, 512], F32, tag="o", name="po%d" % it)
            for f0, fn in FSPLIT:
                for g in range(2):
                    a0 = 256 * it + 128 * g
                    nc.tensor.matmul_mx(
                        out=po[:, f0 : f0 + fn],
                        lhsT=aq[:, a0 : a0 + 128].bitcast(FP8X4),
                        lhsT_scale=asc[:, a0 : a0 + 128],
                        rhs=hq[:, F * g + f0 : F * g + f0 + fn].bitcast(FP8X4),
                        rhs_scale=hsc[:, F * g + f0 : F * g + f0 + fn],
                        start=(g == 0),
                        stop=(g == 1),
                    )
            pos[it] = po

        def e1(it):
            s = keep.tile([P, F], F32, name="s%d" % it)
            nc.vector.scalar_tensor_tensor(
                out=s[:], in0=T[:, it, :], scalar=dinv[:, it : it + 1], in1=pos[it][:, 0:F],
                op0=ALU.mult, op1=ALU.add,
            )
            ss[it] = s

        def eg(it):
            gl = keep.tile([P, F], F32, name="gl%d" % it)
            nc.scalar.activation(
                out=gl[:], in_=ss[it][:], func=ACT.Gelu, scale=dinv[:, it : it + 1], accum_out=sumg[:, it : it + 1],
            )
            gls[it] = gl

        def emu(it):
            nc.gpsimd.tensor_scalar(
                out=negmu[:, it : it + 1], in0=sumg[:, it : it + 1], scalar1=-1.0 / F, scalar2=0.0,
                op0=ALU.mult, op1=ALU.add,
            )

        def eq(it):
            sq = junk.tile([P, F], F32, tag="sq", name="sq%d" % it)
            nc.scalar.activation(
                out=sq[:], in_=gls[it][:], func=ACT.Square, scale=-float(F), bias=sumg[:, it : it + 1],
                accum_out=ssq[:, it : it + 1],
            )

        def er(h):
            cols = slice(2 * h, 2 * h + 2)
            nc.gpsimd.tensor_scalar(
                out=vare[:, cols], in0=ssq[:, cols], scalar1=1.0 / (float(F) ** 3), scalar2=EPS,
                op0=ALU.mult, op1=ALU.add,
            )
            nc.gpsimd.tensor_tensor(out=rstd[:, cols], in0=vare[:, cols], in1=neghalf[:, 0:2], op=ALU.pow)

        def e4(it):
            w = keep.tile([P, F], F32, name="w%d" % it)
            nc.vector.scalar_tensor_tensor(
                out=w[:], in0=gls[it][:], scalar=negmu[:, it : it + 1], in1=gb[:, 0:F],
                op0=ALU.add, op1=ALU.mult,
            )
            ws[it] = w

        def e5(it):
            o = keep.tile([P, F], F32, name="o%d" % it)
            nc.vector.scalar_tensor_tensor(
                out=o[:], in0=ws[it][:], scalar=rstd[:, it : it + 1], in1=gb[:, 512 : 512 + F],
                op0=ALU.mult, op1=ALU.add,
            )
            nc.sync.dma_start(out=out_v[:, it // 2, it % 2, :], in_=o[:])

        def e5s(it):
            for f0, fn in FSPLIT:
                o = keep.tile([P, fn], F32, name="o%d_%d" % (it, f0))
                nc.vector.scalar_tensor_tensor(
                    out=o[:], in0=ws[it][:, f0 : f0 + fn], scalar=rstd[:, it : it + 1], in1=gb[:, 512 + f0 : 512 + f0 + fn],
                    op0=ALU.mult, op1=ALU.add,
                )
                nc.sync.dma_start(out=out_v[:, it // 2, it % 2, f0 : f0 + fn], in_=o[:])

        def lg(v):
            nc.sync.dma_start(out=vec[0:1, v, 0:F], in_=(ln_gamma if v == 1 else ln_beta).unsqueeze(0))

        lx(0); lw(); lx(1); lx(2); lah(0, 1); lx(3); lah(0, 0); la(1); la(2); la(3); lg(1); lg(2)
        xT(0); xT(1); xe(0); w1s_(256, 128); xe(1); xT(2); xe(2); bcm(0); bce(0); xT(3); xe(3)
        w1v(0, 256); xqz(0); w1qz(); xqz(1); mm1(0); mm1(1); mm1(2); mm1(3)
        degv(1); xqz(2); tp(0); xqz(3); tp(1)
        aT(0); mm1(4); mm1(5); mm1(6); mm1(7)
        degs(0); degs(2); degv(3); drs(0)
        tp(2); tp(3); hg(0); hg(1); hg(2); hg(3)
        tp(4); tp(5); degv(5); tp(6); tp(7); degv(7)
        ae(0); degs(4); degs(6)
        aT(1); aT(2); aT(3); aT(4); aT(5)
        ae(1); drs(1); ae(2); aT(6); aT(7); bcm(1); bcm(2)
        nc.scalar.activation(out=warm2[:], in_=ones_f[:, 0:1], func=ACT.Gelu)
        ae(3); ae(4); ae(5); ae(6); ae(7)
        il(); aqz(0); hqz(0); f2(1); aqz(1); hqz(1)
        aqz(2); aqz(3)


        for p in range(NT + LAG5):
            if p < NT:
                mm2(p); e1(p); eg(p); emu(p)
            if p + 4 < NT:
                aqz(p + 4)
            if 0 <= p - 1 < NT:
                eq(p - 1)
                if p % 2 == 0:
                    er(p // 2 - 1)
            if 0 <= p - LAG4 < NT:
                e4(p - LAG4)
            if 0 <= p - LAG5 < NT - 1:
                e5(p - LAG5)
        e5s(NT - 1)
